import numpy as np
import ml_dtypes


def mxq(x, axis, fmt="e4m3"):
    dtype, down = {"e4m3": (ml_dtypes.float8_e4m3fn, 7), "e5m2": (ml_dtypes.float8_e5m2, 14)}[fmt]
    v = np.moveaxis(np.asarray(x, np.float32).astype(ml_dtypes.bfloat16).astype(np.float64), axis, -1)
    blocks = v.reshape(v.shape[:-1] + (-1, 32))
    amax = np.abs(blocks).max(-1, keepdims=True)
    byte = np.maximum(np.where(amax > 0, np.frexp(amax)[1] - 1 + 127, 0) - down, 1)
    scale = np.exp2(byte - 127.0)
    codes = (blocks / scale).astype(np.float32).astype(dtype).astype(np.float64)
    return np.moveaxis((codes * scale).reshape(v.shape), -1, axis)


WIDE = False


def mx_kscale(k):
    if not WIDE:
        return np.ones(k)
    levels = np.array([10, -10, 5, -5, 0])
    a = np.random.permutation(np.resize(levels, k // 512 * 4)).reshape(k // 512, 4)
    idx = np.arange(k)
    return np.exp2(a[idx // 512, idx % 128 // 32])


BF16 = ml_dtypes.bfloat16


def bf(x):
    return np.asarray(x, np.float32).astype(BF16)


def f64(x):
    return np.asarray(x).astype(np.float64)


E2M1 = np.array([0.0, 0.5, 1.0, 1.5, 2.0, 3.0, 4.0, 6.0, -0.0, -0.5, -1.0, -1.5, -2.0, -3.0, -4.0, -6.0])


def pack_weight(w, fmt):
    k, n = w.shape
    w = f64(bf(w)).reshape(k // 32, 32, n)
    amax = np.abs(w).max(1)
    if fmt == "e4m3":
        byte = np.frexp(amax)[1] - 1 + 127 - 7
    else:
        mant, ex = np.frexp(amax / 6.0)
        byte = np.where(mant > 0.5, ex, ex - 1) + 127
    byte = np.clip(np.where(amax > 0, byte, 1), 1, 254)
    scaled = (w * np.exp2(127.0 - byte)[:, None, :]).reshape(k, n).astype(np.float32)
    by_word = np.ascontiguousarray(scaled.reshape(k // 512, 128, 4, n).transpose(0, 1, 3, 2))
    if fmt == "e4m3":
        words = by_word.astype(ml_dtypes.float8_e4m3fn).view(np.uint8)
    else:
        c = by_word.astype(ml_dtypes.float4_e2m1fn).view(np.uint8) & 0xF
        words = c[..., 0::2] | (c[..., 1::2] << 4)
    return np.ascontiguousarray(words), np.ascontiguousarray(byte.astype(np.uint8).reshape(k // 512, 16, n))


def unpack_weight(words, scales, fmt):
    g, p, n, _ = words.shape
    if fmt == "e4m3":
        vals = np.ascontiguousarray(words).view(ml_dtypes.float8_e4m3fn).astype(np.float64)
    else:
        nib = np.empty((g, p, n, 4), np.uint8)
        nib[..., 0::2] = words & 0xF
        nib[..., 1::2] = words >> 4
        vals = E2M1[nib]
    vals = vals * np.repeat(np.exp2(scales.astype(np.float64) - 127.0), 8, axis=1)[..., None]
    return vals.transpose(0, 1, 3, 2).reshape(g * 512, n)


T, B, I, H = 32, 128, 512, 512


def sigmoid(v):
    return 1.0 / (1.0 + np.exp(-v))


def setup_inputs():
    s = mx_kscale(I)
    inp = bf(np.random.standard_normal((T, B, I)) * s)
    h0 = bf(np.random.standard_normal((B, H)))
    c0 = bf(np.random.standard_normal((B, H)))
    noise = bf(np.random.standard_normal((B, H)) * 0.3)
    w_ih = np.random.standard_normal((4 * H, I)) / np.sqrt(I) / s[None, :]
    words, scales = pack_weight(np.ascontiguousarray(w_ih.T), "e4m3")
    return {
        "input": inp,
        "h0": h0,
        "c0": c0,
        "noise": noise,
        "W_ih_words": words,
        "W_ih_scales": scales,
        "W_hh": bf(np.random.standard_normal((4 * H, H)) * 0.7 / np.sqrt(H)),
        "b_ih": bf(np.random.standard_normal(4 * H) * 0.3),
        "b_hh": bf(np.random.standard_normal(4 * H) * 0.3),
    }


def reference(input, h0, c0, noise, W_ih_words, W_ih_scales, W_hh, b_ih, b_hh):
    hsz = h0.shape[-1]
    gx = mxq(f64(input), 2, "e4m3") @ unpack_weight(W_ih_words, W_ih_scales, "e4m3")
    gh = f64(h0) @ f64(W_hh).T
    gates = gx + gh[None, :, :] + (f64(b_ih) + f64(b_hh))
    i_g = sigmoid(gates[..., 0 * hsz:1 * hsz])
    f_g = sigmoid(gates[..., 1 * hsz:2 * hsz])
    g_g = np.tanh(gates[..., 2 * hsz:3 * hsz])
    o_g = sigmoid(gates[..., 3 * hsz:4 * hsz])
    c = f_g * f64(c0)[None] + i_g * g_g
    h = o_g * np.tanh(c) + f64(noise)[None]
    return (h, np.stack([h[-1], c[-1]]))

@@ -1,0 +1,201 @@
+from contextlib import ExitStack
+
+import concourse.mybir as mybir
+from concourse.masks import make_identity
+
+F32 = mybir.dt.float32
+BF16 = mybir.dt.bfloat16
+U8 = mybir.dt.uint8
+U32 = mybir.dt.uint32
+I32 = mybir.dt.int32
+FP8X4 = mybir.dt.float8_e4m3fn_x4
+ACT = mybir.ActivationFunctionType
+ALU = mybir.AluOpType
+
+T = 32
+P = 128
+K = 512
+H = 512
+GATES = 4
+N = GATES * H
+WORDS = K // 2
+H_CHUNKS = H // P
+ROW_BLOCKS = H // P
+STEPS = 2
+LOAD_STEPS = 4
+
+FLOPS = 2 * T * P * K * N + 2 * P * H * N
+
+
+def tile_lstmlayer_kernel(
+    tc, x, h0, c0, noise, w_ih_words, w_ih_scales, w_hh, b_ih, b_hh, h_out, state_out
+):
+    nc = tc.nc
+    with ExitStack() as ctx:
+        keep = ctx.enter_context(tc.tile_pool(name="keep", bufs=1))
+        stage = ctx.enter_context(tc.tile_pool(name="stage", bufs=3))
+        work = ctx.enter_context(tc.tile_pool(name="work", bufs=3))
+        parked_psum = ctx.enter_context(tc.psum_pool(name="parked_psum", bufs=1))
+        turned_psum = ctx.enter_context(tc.psum_pool(name="turned_psum", bufs=2))
+        product_psum = ctx.enter_context(tc.psum_pool(name="product_psum", bufs=4))
+
+        ident_bf16 = keep.tile([P, P], BF16)
+        make_identity(nc, ident_bf16[:])
+        ident_f32 = keep.tile([P, P], F32)
+        make_identity(nc, ident_f32[:])
+        ones = keep.tile([P, P], BF16)
+        nc.vector.memset(ones[:], 1.0)
+        bias_rows = keep.tile([P, N], BF16)
+        nc.vector.memset(bias_rows[:], 0.0)
+        w_scales = keep.tile([P, N], U8, align_bytes=64)
+        nc.vector.memset(w_scales[:].bitcast(I32), 0)
+
+        h0_sb = keep.tile([P, H], BF16)
+        nc.sync.dma_start(out=h0_sb[:], in_=h0)
+        whh_sb = keep.tile([P, GATES * ROW_BLOCKS, H], BF16)
+        w_codes = keep.tile([P, N], U32, align_bytes=64)
+        w_words_flat = w_ih_words[0].rearrange("p n t -> p (n t)").bitcast(I32)
+        x_sb = keep.tile([P, T, K], BF16)
+
+        def load_whh(g):
+            nc.sync.dma_start(
+                out=whh_sb[:, g * ROW_BLOCKS : (g + 1) * ROW_BLOCKS, :],
+                in_=w_hh[g * H : (g + 1) * H, :].rearrange("(j p) k -> p j k", p=P),
+            )
+
+        def load_w_codes(g):
+            nc.sync.dma_start(
+                out=w_codes[:, g * H : (g + 1) * H].bitcast(I32),
+                in_=w_words_flat[:, g * H : (g + 1) * H],
+            )
+
+        def load_x(first):
+            nc.sync.dma_start(
+                out=x_sb[:, first : first + LOAD_STEPS, :],
+                in_=x[first : first + LOAD_STEPS].rearrange("t b k -> b t k"),
+            )
+
+        load_whh(0)
+        nc.sync.dma_start(out=bias_rows[0:1, :], in_=b_ih.rearrange("(o n) -> o n", o=1))
+        nc.sync.dma_start(out=bias_rows[1:2, :], in_=b_hh.rearrange("(o n) -> o n", o=1))
+        for quadrant in range(4):
+            nc.sync.dma_start(
+                out=w_scales[32 * quadrant : 32 * quadrant + 4, :].bitcast(I32),
+                in_=w_ih_scales[0, 4 * quadrant : 4 * quadrant + 4, :].bitcast(I32),
+            )
+        load_x(0)
+        load_w_codes(0)
+        for g in range(1, GATES):
+            load_whh(g)
+            load_w_codes(g)
+        c0_sb = keep.tile([P, H], BF16)
+        nc.sync.dma_start(out=c0_sb[:], in_=c0)
+        noise_sb = keep.tile([P, H], BF16)
+        nc.sync.dma_start(out=noise_sb[:], in_=noise)
+        for first in range(LOAD_STEPS, T, LOAD_STEPS):
+            load_x(first)
+
+        h0_turned = turned_psum.tile([P, H_CHUNKS, P], BF16, tag="turned")
+        for c in range(H_CHUNKS):
+            nc.tensor.transpose(h0_turned[:, c, :], h0_sb[:, c * P : (c + 1) * P], ident_bf16[:])
+        h0T = keep.tile([P, H_CHUNKS, P], BF16)
+        nc.vector.tensor_copy(out=h0T[:], in_=h0_turned[:])
+
+        whhT = keep.tile([P, H_CHUNKS, N], BF16)
+        fixed = keep.tile([P, GATES, H], F32)
+        for g in range(GATES):
+            cols = slice(g * H, (g + 1) * H)
+            for pair in range(H_CHUNKS // 2):
+                whh_turned = turned_psum.tile([P, 2, H], BF16, tag="turned")
+                for c in range(2):
+                    chunk = 2 * pair + c
+                    for j in range(ROW_BLOCKS):
+                        nc.tensor.transpose(
+                            whh_turned[:, c, j * P : (j + 1) * P],
+                            whh_sb[:, g * ROW_BLOCKS + j, chunk * P : (chunk + 1) * P],
+                            ident_bf16[:],
+                        )
+                if pair == 0:
+                    nc.vector.tensor_copy(out=whhT[:, 0:2, cols], in_=whh_turned[:])
+                else:
+                    nc.scalar.copy(out=whhT[:, 2:4, cols], in_=whh_turned[:])
+            fixed_sum = product_psum.tile([P, H], F32, tag="product")
+            for c in range(H_CHUNKS):
+                nc.tensor.matmul(
+                    fixed_sum[:], lhsT=h0T[:, c, :], rhs=whhT[:, c, cols], start=(c == 0), stop=False
+                )
+            nc.tensor.matmul(
+                fixed_sum[:], lhsT=ones[:], rhs=bias_rows[:, cols], start=False, stop=True
+            )
+            nc.scalar.copy(out=fixed[:, g, :], in_=fixed_sum[:])
+
+        c0_parked = parked_psum.tile([P, H], F32)
+        nc.tensor.matmul(c0_parked[:], lhsT=ident_bf16[:], rhs=c0_sb[:], start=True, stop=True)
+        noise_parked = parked_psum.tile([P, H], F32)
+        nc.tensor.matmul(noise_parked[:], lhsT=ident_bf16[:], rhs=noise_sb[:], start=True, stop=True)
+        c0_each_step = c0_parked[:].unsqueeze(1).to_broadcast([P, STEPS, H])
+        noise_each_step = noise_parked[:].unsqueeze(1).to_broadcast([P, STEPS, H])
+
+        x_words = x_sb[:].rearrange("b t k -> b (t k)").bitcast(F32)
+        for first in range(0, T, STEPS):
+            turned = turned_psum.tile([P, STEPS, 2, P], F32, tag="turned")
+            for s in range(STEPS):
+                row = (first + s) * WORDS
+                for u in range(2):
+                    nc.tensor.transpose(
+                        turned[:, s, u, :], x_words[:, row + u : row + WORDS : 2], ident_f32[:]
+                    )
+            grouped = stage.tile([P, STEPS * K], BF16, align_bytes=64)
+            nc.scalar.copy(
+                out=grouped[:].bitcast(F32).rearrange("p (s b u) -> p s b u", s=STEPS, u=2),
+                in_=turned[:].rearrange("p s u b -> p s b u"),
+            )
+            x_codes = stage.tile([P, STEPS * P], U32, align_bytes=64)
+            x_scales = stage.tile([P, STEPS * P], U8, align_bytes=64)
+            nc.vector.quantize_mx(
+                out=x_codes[:].bitcast(FP8X4), scales=x_scales[:], in_=grouped[:]
+            )
+
+            gates = work.tile([P, GATES, STEPS, H], F32)
+            for g in range(GATES):
+                cols = slice(g * H, (g + 1) * H)
+                for s in range(STEPS):
+                    rows = slice(s * P, (s + 1) * P)
+                    product = product_psum.tile([P, H], F32, tag="product")
+                    nc.tensor.matmul_mx(
+                        out=product[:],
+                        lhsT=x_codes[:, rows].bitcast(FP8X4),
+                        lhsT_scale=x_scales[:, rows],
+                        rhs=w_codes[:, cols].bitcast(FP8X4),
+                        rhs_scale=w_scales[:, cols],
+                        start=True,
+                        stop=True,
+                    )
+                    nc.vector.tensor_tensor(
+                        out=gates[:, g, s, :], in0=product[:], in1=fixed[:, g, :], op=ALU.add
+                    )
+
+            nc.scalar.activation(out=gates[:, 0:2], in_=gates[:, 0:2], func=ACT.Sigmoid)
+            nc.scalar.activation(out=gates[:, 2], in_=gates[:, 2], func=ACT.Tanh)
+            nc.scalar.activation(out=gates[:, 3], in_=gates[:, 3], func=ACT.Sigmoid)
+
+            kept = work.tile([P, STEPS, H], F32)
+            nc.vector.tensor_tensor(out=kept[:], in0=gates[:, 1], in1=c0_each_step, op=ALU.mult)
+            fresh = work.tile([P, STEPS, H], F32)
+            nc.gpsimd.tensor_tensor(out=fresh[:], in0=gates[:, 0], in1=gates[:, 2], op=ALU.mult)
+            cell = work.tile([P, STEPS, H], F32)
+            nc.gpsimd.tensor_tensor(out=cell[:], in0=kept[:], in1=fresh[:], op=ALU.add)
+
+            squashed = work.tile([P, STEPS, H], F32)
+            nc.scalar.activation(out=squashed[:], in_=cell[:], func=ACT.Tanh)
+            shown = work.tile([P, STEPS, H], F32)
+            nc.gpsimd.tensor_tensor(out=shown[:], in0=gates[:, 3], in1=squashed[:], op=ALU.mult)
+            hidden = work.tile([P, STEPS, H], F32)
+            nc.vector.tensor_tensor(out=hidden[:], in0=shown[:], in1=noise_each_step, op=ALU.add)
+
+            nc.sync.dma_start(
+                out=h_out[first : first + STEPS].rearrange("t b n -> b t n"), in_=hidden[:]
+            )
+            if first + STEPS == T:
+                nc.sync.dma_start(out=state_out[0], in_=hidden[:, STEPS - 1, :])
+                nc.sync.dma_start(out=state_out[1], in_=cell[:, STEPS - 1, :])

@@ -17,11 +17,18 @@ P = 128
 K = 512
 H = 512
 GATES = 4
+GATE_I = 0
+GATE_F = 1
+GATE_G = 2
+GATE_O = 3
+GATE_ORDER = (GATE_I, GATE_G, GATE_F, GATE_O)
+GATE_FUNC = {GATE_I: ACT.Sigmoid, GATE_F: ACT.Sigmoid, GATE_G: ACT.Tanh, GATE_O: ACT.Sigmoid}
 N = GATES * H
 WORDS = K // 2
 H_CHUNKS = H // P
 ROW_BLOCKS = H // P
 STEPS = 2
+ROUNDS = T // STEPS
 LOAD_STEPS = 4
 
 FLOPS = 2 * T * P * K * N + 2 * P * H * N
@@ -32,6 +39,7 @@ def tile_lstmlayer_kernel(
 ):
     nc = tc.nc
     with ExitStack() as ctx:
+        ctx.enter_context(tc.manual_schedule())
         keep = ctx.enter_context(tc.tile_pool(name="keep", bufs=1))
         stage = ctx.enter_context(tc.tile_pool(name="stage", bufs=3))
         work = ctx.enter_context(tc.tile_pool(name="work", bufs=3))
@@ -51,7 +59,8 @@ def tile_lstmlayer_kernel(
         nc.vector.memset(w_scales[:].bitcast(I32), 0)
 
         h0_sb = keep.tile([P, H], BF16)
-        nc.sync.dma_start(out=h0_sb[:], in_=h0)
+        c0_sb = keep.tile([P, H], BF16)
+        noise_sb = keep.tile([P, H], BF16)
         whh_sb = keep.tile([P, GATES * ROW_BLOCKS, H], BF16)
         w_codes = keep.tile([P, N], U32, align_bytes=64)
         w_words_flat = w_ih_words[0].rearrange("p n t -> p (n t)").bitcast(I32)
@@ -75,35 +84,41 @@ def tile_lstmlayer_kernel(
                 in_=x[first : first + LOAD_STEPS].rearrange("t b k -> b t k"),
             )
 
-        load_whh(0)
+        nc.sync.dma_start(out=h0_sb[:], in_=h0)
+        load_whh(GATE_ORDER[0])
+        load_whh(GATE_ORDER[1])
+        nc.sync.dma_start(out=c0_sb[:], in_=c0)
+        nc.sync.dma_start(out=noise_sb[:], in_=noise)
         nc.sync.dma_start(out=bias_rows[0:1, :], in_=b_ih.rearrange("(o n) -> o n", o=1))
         nc.sync.dma_start(out=bias_rows[1:2, :], in_=b_hh.rearrange("(o n) -> o n", o=1))
+        load_x(0)
         for quadrant in range(4):
             nc.sync.dma_start(
                 out=w_scales[32 * quadrant : 32 * quadrant + 4, :].bitcast(I32),
                 in_=w_ih_scales[0, 4 * quadrant : 4 * quadrant + 4, :].bitcast(I32),
             )
-        load_x(0)
-        load_w_codes(0)
-        for g in range(1, GATES):
-            load_whh(g)
-            load_w_codes(g)
-        c0_sb = keep.tile([P, H], BF16)
-        nc.sync.dma_start(out=c0_sb[:], in_=c0)
-        noise_sb = keep.tile([P, H], BF16)
-        nc.sync.dma_start(out=noise_sb[:], in_=noise)
+        load_w_codes(GATE_ORDER[0])
+        load_w_codes(GATE_ORDER[1])
+        load_whh(GATE_ORDER[2])
+        load_whh(GATE_ORDER[3])
+        load_w_codes(GATE_ORDER[2])
+        load_w_codes(GATE_ORDER[3])
         for first in range(LOAD_STEPS, T, LOAD_STEPS):
             load_x(first)
 
-        h0_turned = turned_psum.tile([P, H_CHUNKS, P], BF16, tag="turned")
-        for c in range(H_CHUNKS):
-            nc.tensor.transpose(h0_turned[:, c, :], h0_sb[:, c * P : (c + 1) * P], ident_bf16[:])
         h0T = keep.tile([P, H_CHUNKS, P], BF16)
-        nc.vector.tensor_copy(out=h0T[:], in_=h0_turned[:])
-
         whhT = keep.tile([P, H_CHUNKS, N], BF16)
         fixed = keep.tile([P, GATES, H], F32)
-        for g in range(GATES):
+
+        def transpose_h0():
+            h0_turned = turned_psum.tile([P, H_CHUNKS, P], BF16, tag="turned")
+            for c in range(H_CHUNKS):
+                nc.tensor.transpose(
+                    h0_turned[:, c, :], h0_sb[:, c * P : (c + 1) * P], ident_bf16[:]
+                )
+            nc.vector.tensor_copy(out=h0T[:], in_=h0_turned[:])
+
+        def transpose_whh(g):
             cols = slice(g * H, (g + 1) * H)
             for pair in range(H_CHUNKS // 2):
                 whh_turned = turned_psum.tile([P, 2, H], BF16, tag="turned")
@@ -119,6 +134,9 @@ def tile_lstmlayer_kernel(
                     nc.vector.tensor_copy(out=whhT[:, 0:2, cols], in_=whh_turned[:])
                 else:
                     nc.scalar.copy(out=whhT[:, 2:4, cols], in_=whh_turned[:])
+
+        def sum_fixed(g):
+            cols = slice(g * H, (g + 1) * H)
             fixed_sum = product_psum.tile([P, H], F32, tag="product")
             for c in range(H_CHUNKS):
                 nc.tensor.matmul(
@@ -129,73 +147,128 @@ def tile_lstmlayer_kernel(
             )
             nc.scalar.copy(out=fixed[:, g, :], in_=fixed_sum[:])
 
+        x_words = x_sb[:].rearrange("b t k -> b (t k)").bitcast(F32)
+        turned, grouped, x_codes, x_scales = {}, {}, {}, {}
+        gates, kept, fresh, cell, squashed, shown, hidden = {}, {}, {}, {}, {}, {}, {}
+
+        def turn_input(r):
+            turned[r] = turned_psum.tile([P, STEPS, 2, P], F32, tag="turned", name="turned")
+            for s in range(STEPS):
+                row = (r * STEPS + s) * WORDS
+                for u in range(2):
+                    nc.tensor.transpose(
+                        turned[r][:, s, u, :], x_words[:, row + u : row + WORDS : 2], ident_f32[:]
+                    )
+
+        def group_input(r):
+            grouped[r] = stage.tile([P, STEPS * K], BF16, align_bytes=64, name="grouped", tag="grouped")
+            nc.scalar.copy(
+                out=grouped[r][:].bitcast(F32).rearrange("p (s b u) -> p s b u", s=STEPS, u=2),
+                in_=turned[r][:].rearrange("p s u b -> p s b u"),
+            )
+
+        def quantise_input(r):
+            x_codes[r] = stage.tile([P, STEPS * P], U32, align_bytes=64, name="x_codes", tag="x_codes")
+            x_scales[r] = stage.tile([P, STEPS * P], U8, align_bytes=64, name="x_scales", tag="x_scales")
+            nc.vector.quantize_mx(
+                out=x_codes[r][:].bitcast(FP8X4), scales=x_scales[r][:], in_=grouped[r][:]
+            )
+
+        def make_gate(r, g):
+            if g == GATE_ORDER[0]:
+                gates[r] = work.tile([P, GATES, STEPS, H], F32, name="gates", tag="gates")
+            cols = slice(g * H, (g + 1) * H)
+            for s in range(STEPS):
+                rows = slice(s * P, (s + 1) * P)
+                product = product_psum.tile([P, H], F32, tag="product")
+                nc.tensor.matmul_mx(
+                    out=product[:],
+                    lhsT=x_codes[r][:, rows].bitcast(FP8X4),
+                    lhsT_scale=x_scales[r][:, rows],
+                    rhs=w_codes[:, cols].bitcast(FP8X4),
+                    rhs_scale=w_scales[:, cols],
+                    start=True,
+                    stop=True,
+                )
+                nc.vector.tensor_tensor(
+                    out=gates[r][:, g, s, :], in0=product[:], in1=fixed[:, g, :], op=ALU.add
+                )
+            nc.scalar.activation(out=gates[r][:, g], in_=gates[r][:, g], func=GATE_FUNC[g])
+
+        def multiply_i_g(r):
+            fresh[r] = work.tile([P, STEPS, H], F32, name="fresh", tag="fresh")
+            nc.gpsimd.tensor_tensor(
+                out=fresh[r][:], in0=gates[r][:, GATE_I], in1=gates[r][:, GATE_G], op=ALU.mult
+            )
+
+        def multiply_f_c0(r):
+            kept[r] = work.tile([P, STEPS, H], F32, name="kept", tag="kept")
+            nc.vector.tensor_tensor(
+                out=kept[r][:], in0=gates[r][:, GATE_F], in1=c0_each_step, op=ALU.mult
+            )
+
+        def add_cell(r):
+            cell[r] = work.tile([P, STEPS, H], F32, name="cell", tag="cell")
+            nc.gpsimd.tensor_tensor(out=cell[r][:], in0=kept[r][:], in1=fresh[r][:], op=ALU.add)
+            if r == ROUNDS - 1:
+                nc.sync.dma_start(out=state_out[1], in_=cell[r][:, STEPS - 1, :])
+
+        def squash_cell(r):
+            squashed[r] = work.tile([P, STEPS, H], F32, name="squashed", tag="squashed")
+            nc.scalar.activation(out=squashed[r][:], in_=cell[r][:], func=ACT.Tanh)
+
+        def multiply_o(r):
+            shown[r] = work.tile([P, STEPS, H], F32, name="shown", tag="shown")
+            nc.gpsimd.tensor_tensor(
+                out=shown[r][:], in0=gates[r][:, GATE_O], in1=squashed[r][:], op=ALU.mult
+            )
+
+        def add_noise_and_store(r):
+            hidden[r] = work.tile([P, STEPS, H], F32, name="hidden", tag="hidden")
+            nc.vector.tensor_tensor(
+                out=hidden[r][:], in0=shown[r][:], in1=noise_each_step, op=ALU.add
+            )
+            nc.sync.dma_start(
+                out=h_out[r * STEPS : (r + 1) * STEPS].rearrange("t b n -> b t n"), in_=hidden[r][:]
+            )
+            if r == ROUNDS - 1:
+                nc.sync.dma_start(out=state_out[0], in_=hidden[r][:, STEPS - 1, :])
+
+        def run(stage_of_round, r):
+            if 0 <= r < ROUNDS:
+                stage_of_round(r)
+
+        transpose_h0()
+        transpose_whh(GATE_ORDER[0])
+        transpose_whh(GATE_ORDER[1])
         c0_parked = parked_psum.tile([P, H], F32)
         nc.tensor.matmul(c0_parked[:], lhsT=ident_bf16[:], rhs=c0_sb[:], start=True, stop=True)
         noise_parked = parked_psum.tile([P, H], F32)
         nc.tensor.matmul(noise_parked[:], lhsT=ident_bf16[:], rhs=noise_sb[:], start=True, stop=True)
         c0_each_step = c0_parked[:].unsqueeze(1).to_broadcast([P, STEPS, H])
         noise_each_step = noise_parked[:].unsqueeze(1).to_broadcast([P, STEPS, H])
+        turn_input(0)
+        group_input(0)
+        quantise_input(0)
+        turn_input(1)
+        group_input(1)
 
-        x_words = x_sb[:].rearrange("b t k -> b (t k)").bitcast(F32)
-        for first in range(0, T, STEPS):
-            turned = turned_psum.tile([P, STEPS, 2, P], F32, tag="turned")
-            for s in range(STEPS):
-                row = (first + s) * WORDS
-                for u in range(2):
-                    nc.tensor.transpose(
-                        turned[:, s, u, :], x_words[:, row + u : row + WORDS : 2], ident_f32[:]
-                    )
-            grouped = stage.tile([P, STEPS * K], BF16, align_bytes=64)
-            nc.scalar.copy(
-                out=grouped[:].bitcast(F32).rearrange("p (s b u) -> p s b u", s=STEPS, u=2),
-                in_=turned[:].rearrange("p s u b -> p s b u"),
-            )
-            x_codes = stage.tile([P, STEPS * P], U32, align_bytes=64)
-            x_scales = stage.tile([P, STEPS * P], U8, align_bytes=64)
-            nc.vector.quantize_mx(
-                out=x_codes[:].bitcast(FP8X4), scales=x_scales[:], in_=grouped[:]
-            )
-
-            gates = work.tile([P, GATES, STEPS, H], F32)
-            for g in range(GATES):
-                cols = slice(g * H, (g + 1) * H)
-                for s in range(STEPS):
-                    rows = slice(s * P, (s + 1) * P)
-                    product = product_psum.tile([P, H], F32, tag="product")
-                    nc.tensor.matmul_mx(
-                        out=product[:],
-                        lhsT=x_codes[:, rows].bitcast(FP8X4),
-                        lhsT_scale=x_scales[:, rows],
-                        rhs=w_codes[:, cols].bitcast(FP8X4),
-                        rhs_scale=w_scales[:, cols],
-                        start=True,
-                        stop=True,
-                    )
-                    nc.vector.tensor_tensor(
-                        out=gates[:, g, s, :], in0=product[:], in1=fixed[:, g, :], op=ALU.add
-                    )
-
-            nc.scalar.activation(out=gates[:, 0:2], in_=gates[:, 0:2], func=ACT.Sigmoid)
-            nc.scalar.activation(out=gates[:, 2], in_=gates[:, 2], func=ACT.Tanh)
-            nc.scalar.activation(out=gates[:, 3], in_=gates[:, 3], func=ACT.Sigmoid)
-
-            kept = work.tile([P, STEPS, H], F32)
-            nc.vector.tensor_tensor(out=kept[:], in0=gates[:, 1], in1=c0_each_step, op=ALU.mult)
-            fresh = work.tile([P, STEPS, H], F32)
-            nc.gpsimd.tensor_tensor(out=fresh[:], in0=gates[:, 0], in1=gates[:, 2], op=ALU.mult)
-            cell = work.tile([P, STEPS, H], F32)
-            nc.gpsimd.tensor_tensor(out=cell[:], in0=kept[:], in1=fresh[:], op=ALU.add)
-
-            squashed = work.tile([P, STEPS, H], F32)
-            nc.scalar.activation(out=squashed[:], in_=cell[:], func=ACT.Tanh)
-            shown = work.tile([P, STEPS, H], F32)
-            nc.gpsimd.tensor_tensor(out=shown[:], in0=gates[:, 3], in1=squashed[:], op=ALU.mult)
-            hidden = work.tile([P, STEPS, H], F32)
-            nc.vector.tensor_tensor(out=hidden[:], in0=shown[:], in1=noise_each_step, op=ALU.add)
-
-            nc.sync.dma_start(
-                out=h_out[first : first + STEPS].rearrange("t b n -> b t n"), in_=hidden[:]
-            )
-            if first + STEPS == T:
-                nc.sync.dma_start(out=state_out[0], in_=hidden[:, STEPS - 1, :])
-                nc.sync.dma_start(out=state_out[1], in_=cell[:, STEPS - 1, :])
+        for n in range(ROUNDS + 2):
+            for position, g in enumerate(GATE_ORDER):
+                if n == 0:
+                    sum_fixed(g)
+                if n < ROUNDS:
+                    make_gate(n, g)
+                if n == 0 and position + 2 < GATES:
+                    transpose_whh(GATE_ORDER[position + 2])
+                if g == GATE_G:
+                    run(multiply_i_g, n)
+                    run(quantise_input, n + 1)
+                if g == GATE_F:
+                    run(squash_cell, n - 1)
+                    run(multiply_o, n - 1)
+            run(turn_input, n + 2)
+            run(add_noise_and_store, n - 2)
+            run(multiply_f_c0, n)
+            run(add_cell, n)
+            run(group_input, n + 2)

@@ -25,11 +25,14 @@ GATE_ORDER = (GATE_I, GATE_G, GATE_F, GATE_O)
 GATE_FUNC = {GATE_I: ACT.Sigmoid, GATE_F: ACT.Sigmoid, GATE_G: ACT.Tanh, GATE_O: ACT.Sigmoid}
 N = GATES * H
 WORDS = K // 2
-H_CHUNKS = H // P
+H_WORDS = H // 2
+WORD_CHUNKS = H_WORDS // P
 ROW_BLOCKS = H // P
 STEPS = 2
 ROUNDS = T // STEPS
 LOAD_STEPS = 4
+VECTOR_ROUNDS = 1
+WARM_UP = 6
 
 FLOPS = 2 * T * P * K * N + 2 * P * H * N
 
@@ -53,6 +56,8 @@ def tile_lstmlayer_kernel(
         make_identity(nc, ident_f32[:])
         ones = keep.tile([P, P], BF16)
         nc.vector.memset(ones[:], 1.0)
+        zeros = keep.tile([P, H], BF16)
+        nc.vector.memset(zeros[:], 0.0)
         bias_rows = keep.tile([P, N], BF16)
         nc.vector.memset(bias_rows[:], 0.0)
         w_scales = keep.tile([P, N], U8, align_bytes=64)
@@ -87,63 +92,71 @@ def tile_lstmlayer_kernel(
         nc.sync.dma_start(out=h0_sb[:], in_=h0)
         load_whh(GATE_ORDER[0])
         load_whh(GATE_ORDER[1])
-        nc.sync.dma_start(out=c0_sb[:], in_=c0)
-        nc.sync.dma_start(out=noise_sb[:], in_=noise)
         nc.sync.dma_start(out=bias_rows[0:1, :], in_=b_ih.rearrange("(o n) -> o n", o=1))
         nc.sync.dma_start(out=bias_rows[1:2, :], in_=b_hh.rearrange("(o n) -> o n", o=1))
         load_x(0)
+        load_whh(GATE_ORDER[2])
+        load_whh(GATE_ORDER[3])
         for quadrant in range(4):
             nc.sync.dma_start(
                 out=w_scales[32 * quadrant : 32 * quadrant + 4, :].bitcast(I32),
                 in_=w_ih_scales[0, 4 * quadrant : 4 * quadrant + 4, :].bitcast(I32),
             )
-        load_w_codes(GATE_ORDER[0])
-        load_w_codes(GATE_ORDER[1])
-        load_whh(GATE_ORDER[2])
-        load_whh(GATE_ORDER[3])
-        load_w_codes(GATE_ORDER[2])
-        load_w_codes(GATE_ORDER[3])
+        for g in GATE_ORDER:
+            load_w_codes(g)
+        nc.sync.dma_start(out=c0_sb[:], in_=c0)
+        nc.sync.dma_start(out=noise_sb[:], in_=noise)
         for first in range(LOAD_STEPS, T, LOAD_STEPS):
             load_x(first)
 
-        h0T = keep.tile([P, H_CHUNKS, P], BF16)
-        whhT = keep.tile([P, H_CHUNKS, N], BF16)
+        h0_words = h0_sb[:].bitcast(F32)
+        whh_words = whh_sb[:].rearrange("p j k -> p (j k)").bitcast(F32)
+        h0T = keep.tile([P, WORD_CHUNKS, 2 * P], BF16)
+        whhT = keep.tile([P, WORD_CHUNKS, 2 * N], BF16)
         fixed = keep.tile([P, GATES, H], F32)
 
         def transpose_h0():
-            h0_turned = turned_psum.tile([P, H_CHUNKS, P], BF16, tag="turned")
-            for c in range(H_CHUNKS):
+            h0_turned = turned_psum.tile([P, WORD_CHUNKS, P], F32, tag="turned")
+            for w in range(WORD_CHUNKS):
                 nc.tensor.transpose(
-                    h0_turned[:, c, :], h0_sb[:, c * P : (c + 1) * P], ident_bf16[:]
+                    h0_turned[:, w, :], h0_words[:, w * P : (w + 1) * P], ident_f32[:]
                 )
-            nc.vector.tensor_copy(out=h0T[:], in_=h0_turned[:])
+            nc.vector.tensor_copy(
+                out=h0T[:].rearrange("q w c -> q (w c)").bitcast(F32),
+                in_=h0_turned[:].rearrange("q w b -> q (w b)"),
+            )
 
         def transpose_whh(g):
-            cols = slice(g * H, (g + 1) * H)
-            for pair in range(H_CHUNKS // 2):
-                whh_turned = turned_psum.tile([P, 2, H], BF16, tag="turned")
-                for c in range(2):
-                    chunk = 2 * pair + c
-                    for j in range(ROW_BLOCKS):
-                        nc.tensor.transpose(
-                            whh_turned[:, c, j * P : (j + 1) * P],
-                            whh_sb[:, g * ROW_BLOCKS + j, chunk * P : (chunk + 1) * P],
-                            ident_bf16[:],
-                        )
-                if pair == 0:
-                    nc.vector.tensor_copy(out=whhT[:, 0:2, cols], in_=whh_turned[:])
-                else:
-                    nc.scalar.copy(out=whhT[:, 2:4, cols], in_=whh_turned[:])
+            for w in range(WORD_CHUNKS):
+                whh_turned = turned_psum.tile([P, ROW_BLOCKS, P], F32, tag="turned")
+                for j in range(ROW_BLOCKS):
+                    first_word = (g * ROW_BLOCKS + j) * H_WORDS + w * P
+                    nc.tensor.transpose(
+                        whh_turned[:, j, :], whh_words[:, first_word : first_word + P], ident_f32[:]
+                    )
+                copy = nc.vector.tensor_copy if w == 0 else nc.scalar.copy
+                copy(
+                    out=whhT[:, w, 2 * g * H : 2 * (g + 1) * H].bitcast(F32),
+                    in_=whh_turned[:].rearrange("q j n -> q (j n)"),
+                )
 
         def sum_fixed(g):
-            cols = slice(g * H, (g + 1) * H)
             fixed_sum = product_psum.tile([P, H], F32, tag="product")
-            for c in range(H_CHUNKS):
-                nc.tensor.matmul(
-                    fixed_sum[:], lhsT=h0T[:, c, :], rhs=whhT[:, c, cols], start=(c == 0), stop=False
-                )
+            for w in range(WORD_CHUNKS):
+                for e in range(2):
+                    nc.tensor.matmul(
+                        fixed_sum[:],
+                        lhsT=h0T[:, w, e : 2 * P : 2],
+                        rhs=whhT[:, w, 2 * g * H + e : 2 * (g + 1) * H : 2],
+                        start=(w == 0 and e == 0),
+                        stop=False,
+                    )
             nc.tensor.matmul(
-                fixed_sum[:], lhsT=ones[:], rhs=bias_rows[:, cols], start=False, stop=True
+                fixed_sum[:],
+                lhsT=ones[:],
+                rhs=bias_rows[:, g * H : (g + 1) * H],
+                start=False,
+                stop=True,
             )
             nc.scalar.copy(out=fixed[:, g, :], in_=fixed_sum[:])
 
@@ -195,9 +208,15 @@ def tile_lstmlayer_kernel(
                 )
             nc.scalar.activation(out=gates[r][:, g], in_=gates[r][:, g], func=GATE_FUNC[g])
 
+        def on_vector(r):
+            return r >= ROUNDS - VECTOR_ROUNDS
+
+        def helper(r):
+            return nc.vector if on_vector(r) else nc.gpsimd
+
         def multiply_i_g(r):
             fresh[r] = work.tile([P, STEPS, H], F32, name="fresh", tag="fresh")
-            nc.gpsimd.tensor_tensor(
+            helper(r).tensor_tensor(
                 out=fresh[r][:], in0=gates[r][:, GATE_I], in1=gates[r][:, GATE_G], op=ALU.mult
             )
 
@@ -209,7 +228,7 @@ def tile_lstmlayer_kernel(
 
         def add_cell(r):
             cell[r] = work.tile([P, STEPS, H], F32, name="cell", tag="cell")
-            nc.gpsimd.tensor_tensor(out=cell[r][:], in0=kept[r][:], in1=fresh[r][:], op=ALU.add)
+            helper(r).tensor_tensor(out=cell[r][:], in0=kept[r][:], in1=fresh[r][:], op=ALU.add)
             if r == ROUNDS - 1:
                 nc.sync.dma_start(out=state_out[1], in_=cell[r][:, STEPS - 1, :])
 
@@ -219,7 +238,7 @@ def tile_lstmlayer_kernel(
 
         def multiply_o(r):
             shown[r] = work.tile([P, STEPS, H], F32, name="shown", tag="shown")
-            nc.gpsimd.tensor_tensor(
+            helper(r).tensor_tensor(
                 out=shown[r][:], in0=gates[r][:, GATE_O], in1=squashed[r][:], op=ALU.mult
             )
 
@@ -238,37 +257,52 @@ def tile_lstmlayer_kernel(
             if 0 <= r < ROUNDS:
                 stage_of_round(r)
 
+        idle_sum = product_psum.tile([P, H], F32, tag="product")
+        for i in range(WARM_UP):
+            nc.tensor.matmul(idle_sum[:], lhsT=ones[:], rhs=zeros[:], start=True, stop=True)
         transpose_h0()
         transpose_whh(GATE_ORDER[0])
         transpose_whh(GATE_ORDER[1])
-        c0_parked = parked_psum.tile([P, H], F32)
-        nc.tensor.matmul(c0_parked[:], lhsT=ident_bf16[:], rhs=c0_sb[:], start=True, stop=True)
-        noise_parked = parked_psum.tile([P, H], F32)
-        nc.tensor.matmul(noise_parked[:], lhsT=ident_bf16[:], rhs=noise_sb[:], start=True, stop=True)
-        c0_each_step = c0_parked[:].unsqueeze(1).to_broadcast([P, STEPS, H])
-        noise_each_step = noise_parked[:].unsqueeze(1).to_broadcast([P, STEPS, H])
         turn_input(0)
         group_input(0)
         quantise_input(0)
         turn_input(1)
         group_input(1)
+        sum_fixed(GATE_ORDER[0])
+        transpose_whh(GATE_ORDER[2])
+        sum_fixed(GATE_ORDER[1])
+        transpose_whh(GATE_ORDER[3])
+        c0_parked = parked_psum.tile([P, H], F32)
+        noise_parked = parked_psum.tile([P, H], F32)
+        c0_each_step = c0_parked[:].unsqueeze(1).to_broadcast([P, STEPS, H])
+        noise_each_step = noise_parked[:].unsqueeze(1).to_broadcast([P, STEPS, H])
 
         for n in range(ROUNDS + 2):
             for position, g in enumerate(GATE_ORDER):
-                if n == 0:
-                    sum_fixed(g)
                 if n < ROUNDS:
                     make_gate(n, g)
                 if n == 0 and position + 2 < GATES:
-                    transpose_whh(GATE_ORDER[position + 2])
-                if g == GATE_G:
+                    sum_fixed(GATE_ORDER[position + 2])
+                if g == GATE_G and not on_vector(n):
                     run(multiply_i_g, n)
-                    run(quantise_input, n + 1)
                 if g == GATE_F:
                     run(squash_cell, n - 1)
-                    run(multiply_o, n - 1)
+                    if not on_vector(n - 1):
+                        run(multiply_o, n - 1)
+                    run(quantise_input, n + 1)
+            if n == 0:
+                nc.tensor.matmul(
+                    c0_parked[:], lhsT=ident_bf16[:], rhs=c0_sb[:], start=True, stop=True
+                )
+                nc.tensor.matmul(
+                    noise_parked[:], lhsT=ident_bf16[:], rhs=noise_sb[:], start=True, stop=True
+                )
             run(turn_input, n + 2)
+            if on_vector(n - 2):
+                run(multiply_o, n - 2)
             run(add_noise_and_store, n - 2)
             run(multiply_f_c0, n)
+            if on_vector(n):
+                run(multiply_i_g, n)
             run(add_cell, n)
             run(group_input, n + 2)

@@ -21,9 +21,10 @@ GATE_I = 0
 GATE_F = 1
 GATE_G = 2
 GATE_O = 3
-GATE_ORDER = (GATE_I, GATE_G, GATE_F, GATE_O)
+TURNED_GATES = (GATE_I, GATE_G, GATE_F)
 GATE_FUNC = {GATE_I: ACT.Sigmoid, GATE_F: ACT.Sigmoid, GATE_G: ACT.Tanh, GATE_O: ACT.Sigmoid}
 N = GATES * H
+CHUNKS = H // P
 WORDS = K // 2
 H_WORDS = H // 2
 WORD_CHUNKS = H_WORDS // P
@@ -44,10 +45,11 @@ def tile_lstmlayer_kernel(
     with ExitStack() as ctx:
         ctx.enter_context(tc.manual_schedule())
         keep = ctx.enter_context(tc.tile_pool(name="keep", bufs=1))
-        stage = ctx.enter_context(tc.tile_pool(name="stage", bufs=3))
-        work = ctx.enter_context(tc.tile_pool(name="work", bufs=3))
+        stage = ctx.enter_context(tc.tile_pool(name="stage", bufs=2))
+        work = ctx.enter_context(tc.tile_pool(name="work", bufs=2))
         parked_psum = ctx.enter_context(tc.psum_pool(name="parked_psum", bufs=1))
-        turned_psum = ctx.enter_context(tc.psum_pool(name="turned_psum", bufs=2))
+        turned_psum = ctx.enter_context(tc.psum_pool(name="turned_psum", bufs=1))
+        cell_psum = ctx.enter_context(tc.psum_pool(name="cell_psum", bufs=2))
         product_psum = ctx.enter_context(tc.psum_pool(name="product_psum", bufs=4))
 
         ident_bf16 = keep.tile([P, P], BF16)
@@ -90,21 +92,23 @@ def tile_lstmlayer_kernel(
             )
 
         nc.sync.dma_start(out=h0_sb[:], in_=h0)
-        load_whh(GATE_ORDER[0])
-        load_whh(GATE_ORDER[1])
+        load_whh(GATE_I)
+        load_whh(GATE_G)
         nc.sync.dma_start(out=bias_rows[0:1, :], in_=b_ih.rearrange("(o n) -> o n", o=1))
         nc.sync.dma_start(out=bias_rows[1:2, :], in_=b_hh.rearrange("(o n) -> o n", o=1))
         load_x(0)
-        load_whh(GATE_ORDER[2])
-        load_whh(GATE_ORDER[3])
         for quadrant in range(4):
             nc.sync.dma_start(
                 out=w_scales[32 * quadrant : 32 * quadrant + 4, :].bitcast(I32),
                 in_=w_ih_scales[0, 4 * quadrant : 4 * quadrant + 4, :].bitcast(I32),
             )
-        for g in GATE_ORDER:
-            load_w_codes(g)
+        load_w_codes(GATE_I)
+        load_w_codes(GATE_G)
+        load_whh(GATE_F)
+        load_w_codes(GATE_F)
         nc.sync.dma_start(out=c0_sb[:], in_=c0)
+        load_whh(GATE_O)
+        load_w_codes(GATE_O)
         nc.sync.dma_start(out=noise_sb[:], in_=noise)
         for first in range(LOAD_STEPS, T, LOAD_STEPS):
             load_x(first)
@@ -113,7 +117,9 @@ def tile_lstmlayer_kernel(
         whh_words = whh_sb[:].rearrange("p j k -> p (j k)").bitcast(F32)
         h0T = keep.tile([P, WORD_CHUNKS, 2 * P], BF16)
         whhT = keep.tile([P, WORD_CHUNKS, 2 * N], BF16)
-        fixed = keep.tile([P, GATES, H], F32)
+        fixedT = keep.tile([P, len(TURNED_GATES), CHUNKS, P], F32)
+        fixed_o = keep.tile([P, H], F32)
+        c0T = keep.tile([P, CHUNKS, P], F32)
 
         def transpose_h0():
             h0_turned = turned_psum.tile([P, WORD_CHUNKS, P], F32, tag="turned")
@@ -128,7 +134,7 @@ def tile_lstmlayer_kernel(
 
         def transpose_whh(g):
             for w in range(WORD_CHUNKS):
-                whh_turned = turned_psum.tile([P, ROW_BLOCKS, P], F32, tag="turned")
+                whh_turned = cell_psum.tile([P, ROW_BLOCKS, P], F32, tag="cell")
                 for j in range(ROW_BLOCKS):
                     first_word = (g * ROW_BLOCKS + j) * H_WORDS + w * P
                     nc.tensor.transpose(
@@ -140,7 +146,30 @@ def tile_lstmlayer_kernel(
                     in_=whh_turned[:].rearrange("q j n -> q (j n)"),
                 )
 
-        def sum_fixed(g):
+        def sum_fixed_turned(g):
+            fixed_sum = product_psum.tile([P, CHUNKS, P], F32, tag="product")
+            for j in range(CHUNKS):
+                n0 = g * H + j * P
+                for w in range(WORD_CHUNKS):
+                    for e in range(2):
+                        nc.tensor.matmul(
+                            fixed_sum[:, j, :],
+                            lhsT=whhT[:, w, 2 * n0 + e : 2 * (n0 + P) : 2],
+                            rhs=h0T[:, w, e : 2 * P : 2],
+                            start=(w == 0 and e == 0),
+                            stop=False,
+                        )
+                nc.tensor.matmul(
+                    fixed_sum[:, j, :],
+                    lhsT=bias_rows[:, n0 : n0 + P],
+                    rhs=ones[:],
+                    start=False,
+                    stop=True,
+                )
+            nc.scalar.copy(out=fixedT[:, TURNED_GATES.index(g)], in_=fixed_sum[:])
+
+        def sum_fixed_o():
+            g = GATE_O
             fixed_sum = product_psum.tile([P, H], F32, tag="product")
             for w in range(WORD_CHUNKS):
                 for e in range(2):
@@ -158,7 +187,19 @@ def tile_lstmlayer_kernel(
                 start=False,
                 stop=True,
             )
-            nc.scalar.copy(out=fixed[:, g, :], in_=fixed_sum[:])
+            nc.scalar.copy(out=fixed_o[:], in_=fixed_sum[:])
+
+        def turn_c0():
+            c0_turned = product_psum.tile([P, CHUNKS, P], F32, tag="product")
+            for j in range(CHUNKS):
+                nc.tensor.matmul(
+                    c0_turned[:, j, :],
+                    lhsT=c0_sb[:, j * P : (j + 1) * P],
+                    rhs=ident_bf16[:],
+                    start=True,
+                    stop=True,
+                )
+            nc.scalar.copy(out=c0T[:], in_=c0_turned[:])
 
         x_words = x_sb[:].rearrange("b t k -> b (t k)").bitcast(F32)
         turned, grouped, x_codes, x_scales = {}, {}, {}, {}
@@ -181,16 +222,47 @@ def tile_lstmlayer_kernel(
             )
 
         def quantise_input(r):
-            x_codes[r] = stage.tile([P, STEPS * P], U32, align_bytes=64, name="x_codes", tag="x_codes")
-            x_scales[r] = stage.tile([P, STEPS * P], U8, align_bytes=64, name="x_scales", tag="x_scales")
+            x_codes[r] = stage.tile(
+                [P, STEPS * P], U32, align_bytes=64, name="x_codes", tag="x_codes", bufs=4
+            )
+            x_scales[r] = stage.tile(
+                [P, STEPS * P], U8, align_bytes=64, name="x_scales", tag="x_scales", bufs=4
+            )
             nc.vector.quantize_mx(
                 out=x_codes[r][:].bitcast(FP8X4), scales=x_scales[r][:], in_=grouped[r][:]
             )
 
-        def make_gate(r, g):
-            if g == GATE_ORDER[0]:
-                gates[r] = work.tile([P, GATES, STEPS, H], F32, name="gates", tag="gates")
-            cols = slice(g * H, (g + 1) * H)
+        def make_turned_gate(r, g):
+            gate = work.tile([P, CHUNKS, STEPS, P], F32, name="gate", tag="gate%d" % g)
+            gates[(r, g)] = gate
+            slot = TURNED_GATES.index(g)
+            for half in range(CHUNKS // 2):
+                product = product_psum.tile([P, H], F32, tag="product")
+                for jj in range(2):
+                    n0 = g * H + (2 * half + jj) * P
+                    nc.tensor.matmul_mx(
+                        out=product[:, jj * STEPS * P : (jj + 1) * STEPS * P],
+                        lhsT=w_codes[:, n0 : n0 + P].bitcast(FP8X4),
+                        lhsT_scale=w_scales[:, n0 : n0 + P],
+                        rhs=x_codes[r][:].bitcast(FP8X4),
+                        rhs_scale=x_scales[r][:],
+                        start=True,
+                        stop=True,
+                    )
+                nc.vector.tensor_tensor(
+                    out=gate[:, 2 * half : 2 * half + 2],
+                    in0=product[:].rearrange("q (j s b) -> q j s b", j=2, s=STEPS),
+                    in1=fixedT[:, slot, 2 * half : 2 * half + 2, :]
+                    .unsqueeze(2)
+                    .to_broadcast([P, 2, STEPS, P]),
+                    op=ALU.add,
+                )
+            flat = gate[:].rearrange("q j s b -> q (j s b)")
+            nc.scalar.activation(out=flat, in_=flat, func=GATE_FUNC[g])
+
+        def add_o(r):
+            gates[(r, GATE_O)] = work.tile([P, STEPS, H], F32, name="gate_o", tag="gate_o")
+            cols = slice(GATE_O * H, (GATE_O + 1) * H)
             for s in range(STEPS):
                 rows = slice(s * P, (s + 1) * P)
                 product = product_psum.tile([P, H], F32, tag="product")
@@ -204,9 +276,13 @@ def tile_lstmlayer_kernel(
                     stop=True,
                 )
                 nc.vector.tensor_tensor(
-                    out=gates[r][:, g, s, :], in0=product[:], in1=fixed[:, g, :], op=ALU.add
+                    out=gates[(r, GATE_O)][:, s, :], in0=product[:], in1=fixed_o[:], op=ALU.add
                 )
-            nc.scalar.activation(out=gates[r][:, g], in_=gates[r][:, g], func=GATE_FUNC[g])
+
+        def activate_o(r):
+            nc.scalar.activation(
+                out=gates[(r, GATE_O)][:], in_=gates[(r, GATE_O)][:], func=GATE_FUNC[GATE_O]
+            )
 
         def on_vector(r):
             return r >= ROUNDS - VECTOR_ROUNDS
@@ -215,35 +291,59 @@ def tile_lstmlayer_kernel(
             return nc.vector if on_vector(r) else nc.gpsimd
 
         def multiply_i_g(r):
-            fresh[r] = work.tile([P, STEPS, H], F32, name="fresh", tag="fresh")
+            fresh[r] = work.tile([P, CHUNKS, STEPS, P], F32, name="fresh", tag="fresh")
             helper(r).tensor_tensor(
-                out=fresh[r][:], in0=gates[r][:, GATE_I], in1=gates[r][:, GATE_G], op=ALU.mult
+                out=fresh[r][:], in0=gates[(r, GATE_I)][:], in1=gates[(r, GATE_G)][:], op=ALU.mult
             )
 
         def multiply_f_c0(r):
-            kept[r] = work.tile([P, STEPS, H], F32, name="kept", tag="kept")
-            nc.vector.tensor_tensor(
-                out=kept[r][:], in0=gates[r][:, GATE_F], in1=c0_each_step, op=ALU.mult
+            kept[r] = work.tile([P, CHUNKS, STEPS, P], F32, name="kept", tag="kept")
+            helper(r).tensor_tensor(
+                out=kept[r][:],
+                in0=gates[(r, GATE_F)][:],
+                in1=c0T[:].unsqueeze(2).to_broadcast([P, CHUNKS, STEPS, P]),
+                op=ALU.mult,
             )
 
-        def add_cell(r):
-            cell[r] = work.tile([P, STEPS, H], F32, name="cell", tag="cell")
-            helper(r).tensor_tensor(out=cell[r][:], in0=kept[r][:], in1=fresh[r][:], op=ALU.add)
-            if r == ROUNDS - 1:
-                nc.sync.dma_start(out=state_out[1], in_=cell[r][:, STEPS - 1, :])
+        def sum_cell(r):
+            for s in range(STEPS):
+                cell[(r, s)] = cell_psum.tile([P, H], F32, tag="cell", name="cell")
+                for j in range(CHUNKS):
+                    cols = slice(j * P, (j + 1) * P)
+                    nc.tensor.matmul(
+                        cell[(r, s)][:, cols],
+                        lhsT=kept[r][:, j, s, :],
+                        rhs=ident_f32[:],
+                        is_transpose=True,
+                        start=True,
+                        stop=False,
+                    )
+                    nc.tensor.matmul(
+                        cell[(r, s)][:, cols],
+                        lhsT=fresh[r][:, j, s, :],
+                        rhs=ident_f32[:],
+                        is_transpose=True,
+                        start=False,
+                        stop=True,
+                    )
 
         def squash_cell(r):
             squashed[r] = work.tile([P, STEPS, H], F32, name="squashed", tag="squashed")
-            nc.scalar.activation(out=squashed[r][:], in_=cell[r][:], func=ACT.Tanh)
+            for s in range(STEPS):
+                nc.scalar.activation(out=squashed[r][:, s, :], in_=cell[(r, s)][:], func=ACT.Tanh)
+            if r == ROUNDS - 1:
+                last_cell = keep.tile([P, H], F32)
+                nc.scalar.copy(out=last_cell[:], in_=cell[(r, STEPS - 1)][:])
+                nc.sync.dma_start(out=state_out[1], in_=last_cell[:])
 
         def multiply_o(r):
             shown[r] = work.tile([P, STEPS, H], F32, name="shown", tag="shown")
             helper(r).tensor_tensor(
-                out=shown[r][:], in0=gates[r][:, GATE_O], in1=squashed[r][:], op=ALU.mult
+                out=shown[r][:], in0=gates[(r, GATE_O)][:], in1=squashed[r][:], op=ALU.mult
             )
 
         def add_noise_and_store(r):
-            hidden[r] = work.tile([P, STEPS, H], F32, name="hidden", tag="hidden")
+            hidden[r] = work.tile([P, STEPS, H], F32, name="hidden", tag="hidden", bufs=3)
             nc.vector.tensor_tensor(
                 out=hidden[r][:], in0=shown[r][:], in1=noise_each_step, op=ALU.add
             )
@@ -261,48 +361,46 @@ def tile_lstmlayer_kernel(
         for i in range(WARM_UP):
             nc.tensor.matmul(idle_sum[:], lhsT=ones[:], rhs=zeros[:], start=True, stop=True)
         transpose_h0()
-        transpose_whh(GATE_ORDER[0])
-        transpose_whh(GATE_ORDER[1])
+        transpose_whh(GATE_I)
+        transpose_whh(GATE_G)
         turn_input(0)
         group_input(0)
         quantise_input(0)
         turn_input(1)
         group_input(1)
-        sum_fixed(GATE_ORDER[0])
-        transpose_whh(GATE_ORDER[2])
-        sum_fixed(GATE_ORDER[1])
-        transpose_whh(GATE_ORDER[3])
-        c0_parked = parked_psum.tile([P, H], F32)
+        sum_fixed_turned(GATE_I)
+        transpose_whh(GATE_F)
+        sum_fixed_turned(GATE_G)
         noise_parked = parked_psum.tile([P, H], F32)
-        c0_each_step = c0_parked[:].unsqueeze(1).to_broadcast([P, STEPS, H])
         noise_each_step = noise_parked[:].unsqueeze(1).to_broadcast([P, STEPS, H])
 
-        for n in range(ROUNDS + 2):
-            for position, g in enumerate(GATE_ORDER):
-                if n < ROUNDS:
-                    make_gate(n, g)
-                if n == 0 and position + 2 < GATES:
-                    sum_fixed(GATE_ORDER[position + 2])
-                if g == GATE_G and not on_vector(n):
-                    run(multiply_i_g, n)
-                if g == GATE_F:
-                    run(squash_cell, n - 1)
-                    if not on_vector(n - 1):
-                        run(multiply_o, n - 1)
-                    run(quantise_input, n + 1)
-            if n == 0:
-                nc.tensor.matmul(
-                    c0_parked[:], lhsT=ident_bf16[:], rhs=c0_sb[:], start=True, stop=True
-                )
-                nc.tensor.matmul(
-                    noise_parked[:], lhsT=ident_bf16[:], rhs=noise_sb[:], start=True, stop=True
-                )
-            run(turn_input, n + 2)
-            if on_vector(n - 2):
-                run(multiply_o, n - 2)
-            run(add_noise_and_store, n - 2)
-            run(multiply_f_c0, n)
-            if on_vector(n):
-                run(multiply_i_g, n)
-            run(add_cell, n)
-            run(group_input, n + 2)
+        for m in range(ROUNDS + 3):
+            run(activate_o, m - 2)
+            run(multiply_f_c0, m - 1)
+            if m < ROUNDS:
+                make_turned_gate(m, GATE_I)
+                if m == 0:
+                    sum_fixed_turned(GATE_F)
+                make_turned_gate(m, GATE_G)
+                if m == 0:
+                    turn_c0()
+                    transpose_whh(GATE_O)
+                make_turned_gate(m, GATE_F)
+                if m == 0:
+                    sum_fixed_o()
+                    nc.tensor.matmul(
+                        noise_parked[:], lhsT=ident_bf16[:], rhs=noise_sb[:], start=True, stop=True
+                    )
+            if on_vector(m - 2):
+                run(add_noise_and_store, m - 3)
+                run(multiply_o, m - 2)
+            else:
+                run(multiply_o, m - 2)
+                run(add_noise_and_store, m - 3)
+            run(quantise_input, m + 1)
+            run(add_o, m - 1)
+            run(sum_cell, m - 1)
+            run(turn_input, m + 2)
+            run(multiply_i_g, m)
+            run(squash_cell, m - 1)
+            run(group_input, m + 2)

@@ -21,10 +21,12 @@ GATE_I = 0
 GATE_F = 1
 GATE_G = 2
 GATE_O = 3
-TURNED_GATES = (GATE_I, GATE_G, GATE_F)
+TURNED_GATES = (GATE_F, GATE_I, GATE_G)
 GATE_FUNC = {GATE_I: ACT.Sigmoid, GATE_F: ACT.Sigmoid, GATE_G: ACT.Tanh, GATE_O: ACT.Sigmoid}
 N = GATES * H
 CHUNKS = H // P
+ALL_CHUNKS = GATES * CHUNKS
+HALVES = 2
 WORDS = K // 2
 H_WORDS = H // 2
 WORD_CHUNKS = H_WORDS // P
@@ -32,6 +34,7 @@ ROW_BLOCKS = H // P
 STEPS = 2
 ROUNDS = T // STEPS
 LOAD_STEPS = 4
+GPSIMD_CHUNKS = 3
 VECTOR_ROUNDS = 1
 WARM_UP = 6
 
@@ -48,36 +51,48 @@ def tile_lstmlayer_kernel(
         stage = ctx.enter_context(tc.tile_pool(name="stage", bufs=2))
         work = ctx.enter_context(tc.tile_pool(name="work", bufs=2))
         parked_psum = ctx.enter_context(tc.psum_pool(name="parked_psum", bufs=1))
-        turned_psum = ctx.enter_context(tc.psum_pool(name="turned_psum", bufs=1))
         cell_psum = ctx.enter_context(tc.psum_pool(name="cell_psum", bufs=2))
         product_psum = ctx.enter_context(tc.psum_pool(name="product_psum", bufs=4))
 
-        ident_bf16 = keep.tile([P, P], BF16)
-        make_identity(nc, ident_bf16[:])
         ident_f32 = keep.tile([P, P], F32)
         make_identity(nc, ident_f32[:])
+        ident_bf16 = keep.tile([P, P], BF16)
+        make_identity(nc, ident_bf16[:])
         ones = keep.tile([P, P], BF16)
         nc.vector.memset(ones[:], 1.0)
         zeros = keep.tile([P, H], BF16)
         nc.vector.memset(zeros[:], 0.0)
-        bias_rows = keep.tile([P, N], BF16)
-        nc.vector.memset(bias_rows[:], 0.0)
         w_scales = keep.tile([P, N], U8, align_bytes=64)
         nc.vector.memset(w_scales[:].bitcast(I32), 0)
+        bias_sb = keep.tile([P, P], BF16)
+        nc.vector.memset(bias_sb[:], 0.0)
+        pick = keep.tile([P, ALL_CHUNKS], BF16)
+        nc.vector.tensor_tensor(
+            out=pick[:],
+            in0=ident_bf16[:, 0:ALL_CHUNKS],
+            in1=ident_bf16[:, ALL_CHUNKS : 2 * ALL_CHUNKS],
+            op=ALU.add,
+        )
 
         h0_sb = keep.tile([P, H], BF16)
         c0_sb = keep.tile([P, H], BF16)
         noise_sb = keep.tile([P, H], BF16)
-        whh_sb = keep.tile([P, GATES * ROW_BLOCKS, H], BF16)
+        whh_sb = {}
         w_codes = keep.tile([P, N], U32, align_bytes=64)
         w_words_flat = w_ih_words[0].rearrange("p n t -> p (n t)").bitcast(I32)
         x_sb = keep.tile([P, T, K], BF16)
 
-        def load_whh(g):
-            nc.sync.dma_start(
-                out=whh_sb[:, g * ROW_BLOCKS : (g + 1) * ROW_BLOCKS, :],
-                in_=w_hh[g * H : (g + 1) * H, :].rearrange("(j p) k -> p j k", p=P),
-            )
+        def load_whh(g, pieces):
+            whh_sb[g] = stage.tile([P, ROW_BLOCKS, H], BF16, name="whh_sb", tag="whh_sb")
+            blocks = ROW_BLOCKS // pieces
+            for piece in range(pieces):
+                first = piece * blocks
+                nc.sync.dma_start(
+                    out=whh_sb[g][:, first : first + blocks, :],
+                    in_=w_hh[g * H + first * P : g * H + (first + blocks) * P, :].rearrange(
+                        "(j p) k -> p j k", p=P
+                    ),
+                )
 
         def load_w_codes(g):
             nc.sync.dma_start(
@@ -85,44 +100,64 @@ def tile_lstmlayer_kernel(
                 in_=w_words_flat[:, g * H : (g + 1) * H],
             )
 
-        def load_x(first):
+        def load_x(first, count):
             nc.sync.dma_start(
-                out=x_sb[:, first : first + LOAD_STEPS, :],
-                in_=x[first : first + LOAD_STEPS].rearrange("t b k -> b t k"),
+                out=x_sb[:, first : first + count, :],
+                in_=x[first : first + count].rearrange("t b k -> b t k"),
             )
 
+        def load_scales(first_gate, gates_loaded):
+            cols = slice(first_gate * H, (first_gate + gates_loaded) * H)
+            for quadrant in range(4):
+                nc.sync.dma_start(
+                    out=w_scales[32 * quadrant : 32 * quadrant + 4, cols].bitcast(I32),
+                    in_=w_ih_scales[0, 4 * quadrant : 4 * quadrant + 4, cols].bitcast(I32),
+                )
+
+        nc.sync.dma_start(
+            out=bias_sb[0:ALL_CHUNKS, :], in_=b_ih.rearrange("(c n) -> c n", c=ALL_CHUNKS)
+        )
+        nc.sync.dma_start(
+            out=bias_sb[ALL_CHUNKS : 2 * ALL_CHUNKS, :], in_=b_hh.rearrange("(c n) -> c n", c=ALL_CHUNKS)
+        )
+        load_x(0, STEPS)
         nc.sync.dma_start(out=h0_sb[:], in_=h0)
-        load_whh(GATE_I)
-        load_whh(GATE_G)
-        nc.sync.dma_start(out=bias_rows[0:1, :], in_=b_ih.rearrange("(o n) -> o n", o=1))
-        nc.sync.dma_start(out=bias_rows[1:2, :], in_=b_hh.rearrange("(o n) -> o n", o=1))
-        load_x(0)
-        for quadrant in range(4):
-            nc.sync.dma_start(
-                out=w_scales[32 * quadrant : 32 * quadrant + 4, :].bitcast(I32),
-                in_=w_ih_scales[0, 4 * quadrant : 4 * quadrant + 4, :].bitcast(I32),
-            )
-        load_w_codes(GATE_I)
-        load_w_codes(GATE_G)
-        load_whh(GATE_F)
+        load_whh(GATE_F, 2)
+        load_x(STEPS, STEPS)
         load_w_codes(GATE_F)
+        load_scales(GATE_F, 1)
         nc.sync.dma_start(out=c0_sb[:], in_=c0)
-        load_whh(GATE_O)
+        load_x(4, LOAD_STEPS)
+        load_whh(GATE_I, 1)
+        load_x(8, LOAD_STEPS)
+        load_w_codes(GATE_I)
+        load_scales(GATE_I, 1)
+        load_whh(GATE_G, 1)
+        load_x(12, LOAD_STEPS)
+        load_w_codes(GATE_G)
+        load_scales(GATE_G, 2)
+        load_x(16, LOAD_STEPS)
+        load_x(20, LOAD_STEPS)
+        load_whh(GATE_O, 1)
+        load_x(24, LOAD_STEPS)
         load_w_codes(GATE_O)
+        load_x(28, LOAD_STEPS)
         nc.sync.dma_start(out=noise_sb[:], in_=noise)
-        for first in range(LOAD_STEPS, T, LOAD_STEPS):
-            load_x(first)
 
         h0_words = h0_sb[:].bitcast(F32)
-        whh_words = whh_sb[:].rearrange("p j k -> p (j k)").bitcast(F32)
         h0T = keep.tile([P, WORD_CHUNKS, 2 * P], BF16)
         whhT = keep.tile([P, WORD_CHUNKS, 2 * N], BF16)
         fixedT = keep.tile([P, len(TURNED_GATES), CHUNKS, P], F32)
         fixed_o = keep.tile([P, H], F32)
         c0T = keep.tile([P, CHUNKS, P], F32)
 
+        def spare_bank(shape, early):
+            if early:
+                return product_psum.tile(shape, F32, tag="product", name="spare")
+            return cell_psum.tile(shape, F32, tag="cell", name="spare")
+
         def transpose_h0():
-            h0_turned = turned_psum.tile([P, WORD_CHUNKS, P], F32, tag="turned")
+            h0_turned = product_psum.tile([P, WORD_CHUNKS, P], F32, tag="product")
             for w in range(WORD_CHUNKS):
                 nc.tensor.transpose(
                     h0_turned[:, w, :], h0_words[:, w * P : (w + 1) * P], ident_f32[:]
@@ -132,81 +167,96 @@ def tile_lstmlayer_kernel(
                 in_=h0_turned[:].rearrange("q w b -> q (w b)"),
             )
 
-        def transpose_whh(g):
+        def transpose_whh(g, half, early=False):
+            whh_words = whh_sb[g][:].rearrange("p j k -> p (j k)").bitcast(F32)
+            blocks = ROW_BLOCKS // HALVES
+            n0 = g * H + half * blocks * P
             for w in range(WORD_CHUNKS):
-                whh_turned = cell_psum.tile([P, ROW_BLOCKS, P], F32, tag="cell")
-                for j in range(ROW_BLOCKS):
-                    first_word = (g * ROW_BLOCKS + j) * H_WORDS + w * P
+                whh_turned = spare_bank([P, blocks, P], early)
+                for jj in range(blocks):
+                    first_word = (half * blocks + jj) * H_WORDS + w * P
                     nc.tensor.transpose(
-                        whh_turned[:, j, :], whh_words[:, first_word : first_word + P], ident_f32[:]
+                        whh_turned[:, jj, :], whh_words[:, first_word : first_word + P], ident_f32[:]
                     )
                 copy = nc.vector.tensor_copy if w == 0 else nc.scalar.copy
                 copy(
-                    out=whhT[:, w, 2 * g * H : 2 * (g + 1) * H].bitcast(F32),
+                    out=whhT[:, w, 2 * n0 : 2 * (n0 + blocks * P)].bitcast(F32),
                     in_=whh_turned[:].rearrange("q j n -> q (j n)"),
                 )
 
-        def sum_fixed_turned(g):
-            fixed_sum = product_psum.tile([P, CHUNKS, P], F32, tag="product")
-            for j in range(CHUNKS):
-                n0 = g * H + j * P
+        def sum_fixed_turned(g, half):
+            chunks = CHUNKS // HALVES
+            fixed_sum = spare_bank([P, chunks, P], False)
+            for jj in range(chunks):
+                n0 = g * H + (half * chunks + jj) * P
                 for w in range(WORD_CHUNKS):
                     for e in range(2):
                         nc.tensor.matmul(
-                            fixed_sum[:, j, :],
+                            fixed_sum[:, jj, :],
                             lhsT=whhT[:, w, 2 * n0 + e : 2 * (n0 + P) : 2],
                             rhs=h0T[:, w, e : 2 * P : 2],
                             start=(w == 0 and e == 0),
                             stop=False,
                         )
+                c = n0 // P
                 nc.tensor.matmul(
-                    fixed_sum[:, j, :],
-                    lhsT=bias_rows[:, n0 : n0 + P],
-                    rhs=ones[:],
+                    fixed_sum[:, jj, :],
+                    lhsT=bias_sb[:],
+                    rhs=pick[:, c : c + 1].to_broadcast([P, P]),
                     start=False,
                     stop=True,
                 )
-            nc.scalar.copy(out=fixedT[:, TURNED_GATES.index(g)], in_=fixed_sum[:])
+            nc.scalar.copy(
+                out=fixedT[:, TURNED_GATES.index(g), half * chunks : (half + 1) * chunks],
+                in_=fixed_sum[:],
+            )
 
         def sum_fixed_o():
-            g = GATE_O
-            fixed_sum = product_psum.tile([P, H], F32, tag="product")
-            for w in range(WORD_CHUNKS):
-                for e in range(2):
-                    nc.tensor.matmul(
-                        fixed_sum[:],
-                        lhsT=h0T[:, w, e : 2 * P : 2],
-                        rhs=whhT[:, w, 2 * g * H + e : 2 * (g + 1) * H : 2],
-                        start=(w == 0 and e == 0),
-                        stop=False,
-                    )
-            nc.tensor.matmul(
-                fixed_sum[:],
-                lhsT=ones[:],
-                rhs=bias_rows[:, g * H : (g + 1) * H],
-                start=False,
-                stop=True,
-            )
-            nc.scalar.copy(out=fixed_o[:], in_=fixed_sum[:])
+            fixed_sum = spare_bank([P, CHUNKS, P], False)
+            for j in range(CHUNKS):
+                n0 = GATE_O * H + j * P
+                for w in range(WORD_CHUNKS):
+                    for e in range(2):
+                        nc.tensor.matmul(
+                            fixed_sum[:, j, :],
+                            lhsT=h0T[:, w, e : 2 * P : 2],
+                            rhs=whhT[:, w, 2 * n0 + e : 2 * (n0 + P) : 2],
+                            start=(w == 0 and e == 0),
+                            stop=False,
+                        )
+                c = n0 // P
+                nc.tensor.matmul(
+                    fixed_sum[:, j, :],
+                    lhsT=pick[:, c : c + 1].to_broadcast([P, P]),
+                    rhs=bias_sb[:],
+                    start=False,
+                    stop=True,
+                )
+            nc.scalar.copy(out=fixed_o[:], in_=fixed_sum[:].rearrange("b j n -> b (j n)"))
 
         def turn_c0():
-            c0_turned = product_psum.tile([P, CHUNKS, P], F32, tag="product")
             for j in range(CHUNKS):
                 nc.tensor.matmul(
-                    c0_turned[:, j, :],
+                    c0_parked[:, j, :],
                     lhsT=c0_sb[:, j * P : (j + 1) * P],
                     rhs=ident_bf16[:],
                     start=True,
                     stop=True,
                 )
-            nc.scalar.copy(out=c0T[:], in_=c0_turned[:])
+            nc.scalar.copy(out=c0T[:, :GPSIMD_CHUNKS], in_=c0_parked[:, :GPSIMD_CHUNKS])
+
+        def park_noise():
+            nc.tensor.matmul(
+                noise_parked[:], lhsT=ident_bf16[:], rhs=noise_sb[:], start=True, stop=True
+            )
 
         x_words = x_sb[:].rearrange("b t k -> b (t k)").bitcast(F32)
         turned, grouped, x_codes, x_scales = {}, {}, {}, {}
-        gates, kept, fresh, cell, squashed, shown, hidden = {}, {}, {}, {}, {}, {}, {}
+        products, gates, cell, squashed = {}, {}, {}, {}
+        GATE_BUFS = {GATE_F: ROUNDS, GATE_I: 3, GATE_G: 2}
 
         def turn_input(r):
-            turned[r] = turned_psum.tile([P, STEPS, 2, P], F32, tag="turned", name="turned")
+            turned[r] = product_psum.tile([P, STEPS, 2, P], F32, tag="product", name="turned")
             for s in range(STEPS):
                 row = (r * STEPS + s) * WORDS
                 for u in range(2):
@@ -223,21 +273,19 @@ def tile_lstmlayer_kernel(
 
         def quantise_input(r):
             x_codes[r] = stage.tile(
-                [P, STEPS * P], U32, align_bytes=64, name="x_codes", tag="x_codes", bufs=4
+                [P, STEPS * P], U32, align_bytes=64, name="x_codes", tag="x_codes", bufs=ROUNDS
             )
             x_scales[r] = stage.tile(
-                [P, STEPS * P], U8, align_bytes=64, name="x_scales", tag="x_scales", bufs=4
+                [P, STEPS * P], U8, align_bytes=64, name="x_scales", tag="x_scales", bufs=ROUNDS
             )
             nc.vector.quantize_mx(
                 out=x_codes[r][:].bitcast(FP8X4), scales=x_scales[r][:], in_=grouped[r][:]
             )
 
-        def make_turned_gate(r, g):
-            gate = work.tile([P, CHUNKS, STEPS, P], F32, name="gate", tag="gate%d" % g)
-            gates[(r, g)] = gate
-            slot = TURNED_GATES.index(g)
-            for half in range(CHUNKS // 2):
-                product = product_psum.tile([P, H], F32, tag="product")
+        def multiply_input_turned(r, g):
+            for half in range(HALVES):
+                product = product_psum.tile([P, H], F32, tag="product", name="product")
+                products[(r, g, half)] = product
                 for jj in range(2):
                     n0 = g * H + (2 * half + jj) * P
                     nc.tensor.matmul_mx(
@@ -249,9 +297,17 @@ def tile_lstmlayer_kernel(
                         start=True,
                         stop=True,
                     )
+
+        def make_turned_gate(r, g):
+            gate = work.tile(
+                [P, CHUNKS, STEPS, P], F32, name="gate", tag="gate%d" % g, bufs=GATE_BUFS[g]
+            )
+            gates[(r, g)] = gate
+            slot = TURNED_GATES.index(g)
+            for half in range(HALVES):
                 nc.vector.tensor_tensor(
                     out=gate[:, 2 * half : 2 * half + 2],
-                    in0=product[:].rearrange("q (j s b) -> q j s b", j=2, s=STEPS),
+                    in0=products[(r, g, half)][:].rearrange("q (j s b) -> q j s b", j=2, s=STEPS),
                     in1=fixedT[:, slot, 2 * half : 2 * half + 2, :]
                     .unsqueeze(2)
                     .to_broadcast([P, 2, STEPS, P]),
@@ -260,14 +316,13 @@ def tile_lstmlayer_kernel(
             flat = gate[:].rearrange("q j s b -> q (j s b)")
             nc.scalar.activation(out=flat, in_=flat, func=GATE_FUNC[g])
 
-        def add_o(r):
-            gates[(r, GATE_O)] = work.tile([P, STEPS, H], F32, name="gate_o", tag="gate_o")
+        def multiply_input_o(r):
             cols = slice(GATE_O * H, (GATE_O + 1) * H)
             for s in range(STEPS):
                 rows = slice(s * P, (s + 1) * P)
-                product = product_psum.tile([P, H], F32, tag="product")
+                products[(r, GATE_O, s)] = product_psum.tile([P, H], F32, tag="product", name="product_o")
                 nc.tensor.matmul_mx(
-                    out=product[:],
+                    out=products[(r, GATE_O, s)][:],
                     lhsT=x_codes[r][:, rows].bitcast(FP8X4),
                     lhsT_scale=x_scales[r][:, rows],
                     rhs=w_codes[:, cols].bitcast(FP8X4),
@@ -275,11 +330,16 @@ def tile_lstmlayer_kernel(
                     start=True,
                     stop=True,
                 )
-                nc.vector.tensor_tensor(
-                    out=gates[(r, GATE_O)][:, s, :], in0=product[:], in1=fixed_o[:], op=ALU.add
-                )
 
-        def activate_o(r):
+        def make_o(r):
+            gates[(r, GATE_O)] = work.tile([P, STEPS, H], F32, name="gate_o", tag="gate_o", bufs=5)
+            for s in range(STEPS):
+                nc.vector.tensor_tensor(
+                    out=gates[(r, GATE_O)][:, s, :],
+                    in0=products[(r, GATE_O, s)][:],
+                    in1=fixed_o[:],
+                    op=ALU.add,
+                )
             nc.scalar.activation(
                 out=gates[(r, GATE_O)][:], in_=gates[(r, GATE_O)][:], func=GATE_FUNC[GATE_O]
             )
@@ -290,18 +350,31 @@ def tile_lstmlayer_kernel(
         def helper(r):
             return nc.vector if on_vector(r) else nc.gpsimd
 
-        def multiply_i_g(r):
-            fresh[r] = work.tile([P, CHUNKS, STEPS, P], F32, name="fresh", tag="fresh")
-            helper(r).tensor_tensor(
-                out=fresh[r][:], in0=gates[(r, GATE_I)][:], in1=gates[(r, GATE_G)][:], op=ALU.mult
+        def multiply_f_c0_on_vector(r):
+            part = gates[(r, GATE_F)][:, GPSIMD_CHUNKS:]
+            nc.vector.tensor_tensor(
+                out=part,
+                in0=part,
+                in1=c0_parked[:, GPSIMD_CHUNKS:, :]
+                .unsqueeze(2)
+                .to_broadcast([P, CHUNKS - GPSIMD_CHUNKS, STEPS, P]),
+                op=ALU.mult,
             )
 
         def multiply_f_c0(r):
-            kept[r] = work.tile([P, CHUNKS, STEPS, P], F32, name="kept", tag="kept")
+            part = gates[(r, GATE_F)][:, :GPSIMD_CHUNKS]
+            nc.gpsimd.tensor_tensor(
+                out=part,
+                in0=part,
+                in1=c0T[:, :GPSIMD_CHUNKS, :].unsqueeze(2).to_broadcast([P, GPSIMD_CHUNKS, STEPS, P]),
+                op=ALU.mult,
+            )
+
+        def multiply_i_g(r):
             helper(r).tensor_tensor(
-                out=kept[r][:],
-                in0=gates[(r, GATE_F)][:],
-                in1=c0T[:].unsqueeze(2).to_broadcast([P, CHUNKS, STEPS, P]),
+                out=gates[(r, GATE_I)][:],
+                in0=gates[(r, GATE_I)][:],
+                in1=gates[(r, GATE_G)][:],
                 op=ALU.mult,
             )
 
@@ -312,7 +385,7 @@ def tile_lstmlayer_kernel(
                     cols = slice(j * P, (j + 1) * P)
                     nc.tensor.matmul(
                         cell[(r, s)][:, cols],
-                        lhsT=kept[r][:, j, s, :],
+                        lhsT=gates[(r, GATE_F)][:, j, s, :],
                         rhs=ident_f32[:],
                         is_transpose=True,
                         start=True,
@@ -320,7 +393,7 @@ def tile_lstmlayer_kernel(
                     )
                     nc.tensor.matmul(
                         cell[(r, s)][:, cols],
-                        lhsT=fresh[r][:, j, s, :],
+                        lhsT=gates[(r, GATE_I)][:, j, s, :],
                         rhs=ident_f32[:],
                         is_transpose=True,
                         start=False,
@@ -328,7 +401,7 @@ def tile_lstmlayer_kernel(
                     )
 
         def squash_cell(r):
-            squashed[r] = work.tile([P, STEPS, H], F32, name="squashed", tag="squashed")
+            squashed[r] = work.tile([P, STEPS, H], F32, name="squashed", tag="squashed", bufs=3)
             for s in range(STEPS):
                 nc.scalar.activation(out=squashed[r][:, s, :], in_=cell[(r, s)][:], func=ACT.Tanh)
             if r == ROUNDS - 1:
@@ -337,70 +410,95 @@ def tile_lstmlayer_kernel(
                 nc.sync.dma_start(out=state_out[1], in_=last_cell[:])
 
         def multiply_o(r):
-            shown[r] = work.tile([P, STEPS, H], F32, name="shown", tag="shown")
             helper(r).tensor_tensor(
-                out=shown[r][:], in0=gates[(r, GATE_O)][:], in1=squashed[r][:], op=ALU.mult
+                out=gates[(r, GATE_O)][:], in0=gates[(r, GATE_O)][:], in1=squashed[r][:], op=ALU.mult
             )
 
         def add_noise_and_store(r):
-            hidden[r] = work.tile([P, STEPS, H], F32, name="hidden", tag="hidden", bufs=3)
             nc.vector.tensor_tensor(
-                out=hidden[r][:], in0=shown[r][:], in1=noise_each_step, op=ALU.add
+                out=gates[(r, GATE_O)][:], in0=gates[(r, GATE_O)][:], in1=noise_each_step, op=ALU.add
             )
             nc.sync.dma_start(
-                out=h_out[r * STEPS : (r + 1) * STEPS].rearrange("t b n -> b t n"), in_=hidden[r][:]
+                out=h_out[r * STEPS : (r + 1) * STEPS].rearrange("t b n -> b t n"),
+                in_=gates[(r, GATE_O)][:],
             )
             if r == ROUNDS - 1:
-                nc.sync.dma_start(out=state_out[0], in_=hidden[r][:, STEPS - 1, :])
+                nc.sync.dma_start(out=state_out[0], in_=gates[(r, GATE_O)][:, STEPS - 1, :])
 
         def run(stage_of_round, r):
             if 0 <= r < ROUNDS:
                 stage_of_round(r)
 
+        noise_parked = parked_psum.tile([P, H], F32)
+        noise_each_step = noise_parked[:].unsqueeze(1).to_broadcast([P, STEPS, H])
+        c0_parked = parked_psum.tile([P, CHUNKS, P], F32)
         idle_sum = product_psum.tile([P, H], F32, tag="product")
         for i in range(WARM_UP):
             nc.tensor.matmul(idle_sum[:], lhsT=ones[:], rhs=zeros[:], start=True, stop=True)
-        transpose_h0()
-        transpose_whh(GATE_I)
-        transpose_whh(GATE_G)
         turn_input(0)
         group_input(0)
+        transpose_h0()
+        transpose_whh(GATE_F, 0)
+        transpose_whh(GATE_F, 1, early=True)
         quantise_input(0)
         turn_input(1)
         group_input(1)
-        sum_fixed_turned(GATE_I)
-        transpose_whh(GATE_F)
-        sum_fixed_turned(GATE_G)
-        noise_parked = parked_psum.tile([P, H], F32)
-        noise_each_step = noise_parked[:].unsqueeze(1).to_broadcast([P, STEPS, H])
+        quantise_input(1)
+        sum_fixed_turned(GATE_F, 0)
+        sum_fixed_turned(GATE_F, 1)
 
+        between = {
+            1: [lambda: transpose_whh(GATE_I, 0)],
+            2: [lambda: transpose_whh(GATE_I, 1)],
+            3: [lambda: sum_fixed_turned(GATE_I, 0)],
+            4: [lambda: sum_fixed_turned(GATE_I, 1)],
+            5: [lambda: transpose_whh(GATE_G, 0)],
+            6: [lambda: transpose_whh(GATE_G, 1)],
+            7: [lambda: sum_fixed_turned(GATE_G, 0)],
+            8: [lambda: sum_fixed_turned(GATE_G, 1)],
+            12: [lambda: transpose_whh(GATE_O, 0)],
+            13: [lambda: transpose_whh(GATE_O, 1)],
+        }
+        for r in range(ROUNDS):
+            multiply_input_turned(r, GATE_F)
+            if r == 0:
+                turn_c0()
+            make_turned_gate(r, GATE_F)
+            if r == 0:
+                turn_input(2)
+                group_input(2)
+            run(turn_input, r + 3)
+            run(group_input, r + 3)
+            if r == 1:
+                quantise_input(2)
+            if r > 0:
+                run(quantise_input, r + 2)
+            for task in between.get(r, []):
+                task()
+            run(multiply_f_c0_on_vector, r - 1)
+            run(multiply_f_c0, r - 1)
+
+        multiply_input_turned(0, GATE_I)
         for m in range(ROUNDS + 3):
-            run(activate_o, m - 2)
-            run(multiply_f_c0, m - 1)
+            run(multiply_i_g, m - 1)
             if m < ROUNDS:
                 make_turned_gate(m, GATE_I)
-                if m == 0:
-                    sum_fixed_turned(GATE_F)
+                multiply_input_turned(m, GATE_G)
                 make_turned_gate(m, GATE_G)
-                if m == 0:
-                    turn_c0()
-                    transpose_whh(GATE_O)
-                make_turned_gate(m, GATE_F)
-                if m == 0:
-                    sum_fixed_o()
-                    nc.tensor.matmul(
-                        noise_parked[:], lhsT=ident_bf16[:], rhs=noise_sb[:], start=True, stop=True
-                    )
+            if m == 0:
+                multiply_f_c0_on_vector(ROUNDS - 1)
+                multiply_f_c0(ROUNDS - 1)
+                sum_fixed_o()
+                park_noise()
+            run(multiply_input_o, m - 1)
+            run(make_o, m - 1)
+            if m + 1 < ROUNDS:
+                multiply_input_turned(m + 1, GATE_I)
+            run(sum_cell, m - 1)
             if on_vector(m - 2):
                 run(add_noise_and_store, m - 3)
                 run(multiply_o, m - 2)
             else:
                 run(multiply_o, m - 2)
                 run(add_noise_and_store, m - 3)
-            run(quantise_input, m + 1)
-            run(add_o, m - 1)
-            run(sum_cell, m - 1)
-            run(turn_input, m + 2)
-            run(multiply_i_g, m)
             run(squash_cell, m - 1)
-            run(group_input, m + 2)

@@ -34,7 +34,7 @@ ROW_BLOCKS = H // P
 STEPS = 2
 ROUNDS = T // STEPS
 LOAD_STEPS = 4
-GPSIMD_CHUNKS = 3
+GPSIMD_CHUNKS = 2
 VECTOR_ROUNDS = 1
 WARM_UP = 6
 

@@ -475,7 +475,6 @@ def tile_lstmlayer_kernel(
                 run(quantise_input, r + 2)
             for task in between.get(r, []):
                 task()
-            run(multiply_f_c0_on_vector, r - 1)
             run(multiply_f_c0, r - 1)
 
         multiply_input_turned(0, GATE_I)
@@ -486,12 +485,12 @@ def tile_lstmlayer_kernel(
                 multiply_input_turned(m, GATE_G)
                 make_turned_gate(m, GATE_G)
             if m == 0:
-                multiply_f_c0_on_vector(ROUNDS - 1)
                 multiply_f_c0(ROUNDS - 1)
                 sum_fixed_o()
                 park_noise()
             run(multiply_input_o, m - 1)
             run(make_o, m - 1)
+            run(multiply_f_c0_on_vector, m)
             if m + 1 < ROUNDS:
                 multiply_input_turned(m + 1, GATE_I)
             run(sum_cell, m - 1)

@@ -114,15 +114,15 @@ def tile_lstmlayer_kernel(
                     in_=w_ih_scales[0, 4 * quadrant : 4 * quadrant + 4, cols].bitcast(I32),
                 )
 
+        load_x(0, STEPS)
+        nc.sync.dma_start(out=h0_sb[:], in_=h0)
+        load_whh(GATE_F, 2)
         nc.sync.dma_start(
             out=bias_sb[0:ALL_CHUNKS, :], in_=b_ih.rearrange("(c n) -> c n", c=ALL_CHUNKS)
         )
         nc.sync.dma_start(
             out=bias_sb[ALL_CHUNKS : 2 * ALL_CHUNKS, :], in_=b_hh.rearrange("(c n) -> c n", c=ALL_CHUNKS)
         )
-        load_x(0, STEPS)
-        nc.sync.dma_start(out=h0_sb[:], in_=h0)
-        load_whh(GATE_F, 2)
         load_x(STEPS, STEPS)
         load_w_codes(GATE_F)
         load_scales(GATE_F, 1)
@@ -178,7 +178,7 @@ def tile_lstmlayer_kernel(
                     nc.tensor.transpose(
                         whh_turned[:, jj, :], whh_words[:, first_word : first_word + P], ident_f32[:]
                     )
-                copy = nc.vector.tensor_copy if w == 0 else nc.scalar.copy
+                copy = nc.scalar.copy if (w == 1 and g == GATE_F) else nc.vector.tensor_copy
                 copy(
                     out=whhT[:, w, 2 * n0 : 2 * (n0 + blocks * P)].bitcast(F32),
                     in_=whh_turned[:].rearrange("q j n -> q (j n)"),
@@ -206,7 +206,8 @@ def tile_lstmlayer_kernel(
                     start=False,
                     stop=True,
                 )
-            nc.scalar.copy(
+            copy = nc.scalar.copy if g == GATE_F else nc.vector.tensor_copy
+            copy(
                 out=fixedT[:, TURNED_GATES.index(g), half * chunks : (half + 1) * chunks],
                 in_=fixed_sum[:],
             )
@@ -298,7 +299,7 @@ def tile_lstmlayer_kernel(
                         stop=True,
                     )
 
-        def make_turned_gate(r, g):
+        def add_turned_gate(r, g):
             gate = work.tile(
                 [P, CHUNKS, STEPS, P], F32, name="gate", tag="gate%d" % g, bufs=GATE_BUFS[g]
             )
@@ -313,7 +314,9 @@ def tile_lstmlayer_kernel(
                     .to_broadcast([P, 2, STEPS, P]),
                     op=ALU.add,
                 )
-            flat = gate[:].rearrange("q j s b -> q (j s b)")
+
+        def activate_turned_gate(r, g):
+            flat = gates[(r, g)][:].rearrange("q j s b -> q (j s b)")
             nc.scalar.activation(out=flat, in_=flat, func=GATE_FUNC[g])
 
         def multiply_input_o(r):
@@ -463,12 +466,15 @@ def tile_lstmlayer_kernel(
             multiply_input_turned(r, GATE_F)
             if r == 0:
                 turn_c0()
-            make_turned_gate(r, GATE_F)
+            add_turned_gate(r, GATE_F)
             if r == 0:
+                activate_turned_gate(r, GATE_F)
                 turn_input(2)
                 group_input(2)
             run(turn_input, r + 3)
             run(group_input, r + 3)
+            if r > 0:
+                activate_turned_gate(r, GATE_F)
             if r == 1:
                 quantise_input(2)
             if r > 0:
@@ -481,9 +487,11 @@ def tile_lstmlayer_kernel(
         for m in range(ROUNDS + 3):
             run(multiply_i_g, m - 1)
             if m < ROUNDS:
-                make_turned_gate(m, GATE_I)
+                add_turned_gate(m, GATE_I)
+                activate_turned_gate(m, GATE_I)
                 multiply_input_turned(m, GATE_G)
-                make_turned_gate(m, GATE_G)
+                add_turned_gate(m, GATE_G)
+                activate_turned_gate(m, GATE_G)
             if m == 0:
                 multiply_f_c0(ROUNDS - 1)
                 sum_fixed_o()

@@ -33,8 +33,9 @@ WORD_CHUNKS = H_WORDS // P
 ROW_BLOCKS = H // P
 STEPS = 2
 ROUNDS = T // STEPS
+PAIRS = ROUNDS // 2
 LOAD_STEPS = 4
-GPSIMD_CHUNKS = 2
+GPSIMD_CHUNKS = (2, 2)
 VECTOR_ROUNDS = 1
 WARM_UP = 6
 
@@ -244,7 +245,7 @@ def tile_lstmlayer_kernel(
                     start=True,
                     stop=True,
                 )
-            nc.scalar.copy(out=c0T[:, :GPSIMD_CHUNKS], in_=c0_parked[:, :GPSIMD_CHUNKS])
+            nc.scalar.copy(out=c0T[:, : max(GPSIMD_CHUNKS)], in_=c0_parked[:, : max(GPSIMD_CHUNKS)])
 
         def park_noise():
             nc.tensor.matmul(
@@ -266,21 +267,29 @@ def tile_lstmlayer_kernel(
                     )
 
         def group_input(r):
-            grouped[r] = stage.tile([P, STEPS * K], BF16, align_bytes=64, name="grouped", tag="grouped")
+            if r % 2 == 0:
+                grouped[r // 2] = stage.tile(
+                    [P, 2, STEPS * K], BF16, align_bytes=64, name="grouped", tag="grouped"
+                )
             nc.scalar.copy(
-                out=grouped[r][:].bitcast(F32).rearrange("p (s b u) -> p s b u", s=STEPS, u=2),
+                out=grouped[r // 2][:, r % 2, :]
+                .bitcast(F32)
+                .rearrange("p (s b u) -> p s b u", s=STEPS, u=2),
                 in_=turned[r][:].rearrange("p s u b -> p s b u"),
             )
 
-        def quantise_input(r):
-            x_codes[r] = stage.tile(
-                [P, STEPS * P], U32, align_bytes=64, name="x_codes", tag="x_codes", bufs=ROUNDS
-            )
-            x_scales[r] = stage.tile(
-                [P, STEPS * P], U8, align_bytes=64, name="x_scales", tag="x_scales", bufs=ROUNDS
-            )
+        def quantise_input(pair, rounds):
+            if pair not in x_codes:
+                x_codes[pair] = stage.tile(
+                    [P, 2, STEPS * P], U32, align_bytes=64, name="x_codes", tag="x_codes", bufs=PAIRS
+                )
+                x_scales[pair] = stage.tile(
+                    [P, 2, STEPS * P], U8, align_bytes=64, name="x_scales", tag="x_scales", bufs=PAIRS
+                )
             nc.vector.quantize_mx(
-                out=x_codes[r][:].bitcast(FP8X4), scales=x_scales[r][:], in_=grouped[r][:]
+                out=x_codes[pair][:, rounds, :].rearrange("p r c -> p (r c)").bitcast(FP8X4),
+                scales=x_scales[pair][:, rounds, :].rearrange("p r c -> p (r c)"),
+                in_=grouped[pair][:, rounds, :].rearrange("p r c -> p (r c)"),
             )
 
         def multiply_input_turned(r, g):
@@ -293,8 +302,8 @@ def tile_lstmlayer_kernel(
                         out=product[:, jj * STEPS * P : (jj + 1) * STEPS * P],
                         lhsT=w_codes[:, n0 : n0 + P].bitcast(FP8X4),
                         lhsT_scale=w_scales[:, n0 : n0 + P],
-                        rhs=x_codes[r][:].bitcast(FP8X4),
-                        rhs_scale=x_scales[r][:],
+                        rhs=x_codes[r // 2][:, r % 2, :].bitcast(FP8X4),
+                        rhs_scale=x_scales[r // 2][:, r % 2, :],
                         start=True,
                         stop=True,
                     )
@@ -326,8 +335,8 @@ def tile_lstmlayer_kernel(
                 products[(r, GATE_O, s)] = product_psum.tile([P, H], F32, tag="product", name="product_o")
                 nc.tensor.matmul_mx(
                     out=products[(r, GATE_O, s)][:],
-                    lhsT=x_codes[r][:, rows].bitcast(FP8X4),
-                    lhsT_scale=x_scales[r][:, rows],
+                    lhsT=x_codes[r // 2][:, r % 2, rows].bitcast(FP8X4),
+                    lhsT_scale=x_scales[r // 2][:, r % 2, rows],
                     rhs=w_codes[:, cols].bitcast(FP8X4),
                     rhs_scale=w_scales[:, cols],
                     start=True,
@@ -354,22 +363,22 @@ def tile_lstmlayer_kernel(
             return nc.vector if on_vector(r) else nc.gpsimd
 
         def multiply_f_c0_on_vector(r):
-            part = gates[(r, GATE_F)][:, GPSIMD_CHUNKS:]
+            first = GPSIMD_CHUNKS[r % 2]
+            part = gates[(r, GATE_F)][:, first:]
             nc.vector.tensor_tensor(
                 out=part,
                 in0=part,
-                in1=c0_parked[:, GPSIMD_CHUNKS:, :]
-                .unsqueeze(2)
-                .to_broadcast([P, CHUNKS - GPSIMD_CHUNKS, STEPS, P]),
+                in1=c0_parked[:, first:, :].unsqueeze(2).to_broadcast([P, CHUNKS - first, STEPS, P]),
                 op=ALU.mult,
             )
 
         def multiply_f_c0(r):
-            part = gates[(r, GATE_F)][:, :GPSIMD_CHUNKS]
+            chunks = GPSIMD_CHUNKS[r % 2]
+            part = gates[(r, GATE_F)][:, :chunks]
             nc.gpsimd.tensor_tensor(
                 out=part,
                 in0=part,
-                in1=c0T[:, :GPSIMD_CHUNKS, :].unsqueeze(2).to_broadcast([P, GPSIMD_CHUNKS, STEPS, P]),
+                in1=c0T[:, :chunks, :].unsqueeze(2).to_broadcast([P, chunks, STEPS, P]),
                 op=ALU.mult,
             )
 
@@ -443,10 +452,10 @@ def tile_lstmlayer_kernel(
         transpose_h0()
         transpose_whh(GATE_F, 0)
         transpose_whh(GATE_F, 1, early=True)
-        quantise_input(0)
+        quantise_input(0, slice(0, 1))
         turn_input(1)
         group_input(1)
-        quantise_input(1)
+        quantise_input(0, slice(1, 2))
         sum_fixed_turned(GATE_F, 0)
         sum_fixed_turned(GATE_F, 1)
 
@@ -469,16 +478,15 @@ def tile_lstmlayer_kernel(
             add_turned_gate(r, GATE_F)
             if r == 0:
                 activate_turned_gate(r, GATE_F)
-                turn_input(2)
-                group_input(2)
-            run(turn_input, r + 3)
-            run(group_input, r + 3)
+            for ahead in ((2, 3), (4, 5))[r] if r < 2 else (r + 4,):
+                run(turn_input, ahead)
+                run(group_input, ahead)
             if r > 0:
                 activate_turned_gate(r, GATE_F)
             if r == 1:
-                quantise_input(2)
-            if r > 0:
-                run(quantise_input, r + 2)
+                quantise_input(1, slice(0, 2))
+            if r % 2 == 0 and 2 <= r and r + 3 < ROUNDS:
+                quantise_input((r + 2) // 2, slice(0, 2))
             for task in between.get(r, []):
                 task()
             run(multiply_f_c0, r - 1)

@@ -63,6 +63,8 @@ def tile_lstmlayer_kernel(
         nc.vector.memset(ones[:], 1.0)
         zeros = keep.tile([P, H], BF16)
         nc.vector.memset(zeros[:], 0.0)
+        table_warmer = keep.tile([P, 1], F32)
+        nc.scalar.activation(out=table_warmer[:], in_=ones[:, 0:1], func=ACT.Sigmoid)
         w_scales = keep.tile([P, N], U8, align_bytes=64)
         nc.vector.memset(w_scales[:].bitcast(I32), 0)
         bias_sb = keep.tile([P, P], BF16)

@@ -51,7 +51,7 @@ def tile_lstmlayer_kernel(
         keep = ctx.enter_context(tc.tile_pool(name="keep", bufs=1))
         stage = ctx.enter_context(tc.tile_pool(name="stage", bufs=2))
         work = ctx.enter_context(tc.tile_pool(name="work", bufs=2))
-        parked_psum = ctx.enter_context(tc.psum_pool(name="parked_psum", bufs=1))
+        parked_psum = ctx.enter_context(tc.psum_pool(name="parked_psum", bufs=2))
         cell_psum = ctx.enter_context(tc.psum_pool(name="cell_psum", bufs=2))
         product_psum = ctx.enter_context(tc.psum_pool(name="product_psum", bufs=4))
 
@@ -238,20 +238,32 @@ def tile_lstmlayer_kernel(
                 )
             nc.scalar.copy(out=fixed_o[:], in_=fixed_sum[:].rearrange("b j n -> b (j n)"))
 
-        def turn_c0():
-            for j in range(CHUNKS):
+        parked = {}
+
+        def turn_c0(bank, chunks):
+            for j in range(chunks):
                 nc.tensor.matmul(
-                    c0_parked[:, j, :],
+                    bank[:, j, :],
                     lhsT=c0_sb[:, j * P : (j + 1) * P],
                     rhs=ident_bf16[:],
                     start=True,
                     stop=True,
                 )
-            nc.scalar.copy(out=c0T[:, : max(GPSIMD_CHUNKS)], in_=c0_parked[:, : max(GPSIMD_CHUNKS)])
+
+        def turn_c0_for_gpsimd():
+            chunks = max(GPSIMD_CHUNKS)
+            bank = spare_bank([P, chunks, P], False)
+            turn_c0(bank, chunks)
+            nc.scalar.copy(out=c0T[:, :chunks], in_=bank[:])
+
+        def park_c0():
+            parked["c0"] = parked_psum.tile([P, CHUNKS, P], F32, tag="parked", name="c0_parked")
+            turn_c0(parked["c0"], CHUNKS)
 
         def park_noise():
+            parked["noise"] = parked_psum.tile([P, H], F32, tag="parked", name="noise_parked")
             nc.tensor.matmul(
-                noise_parked[:], lhsT=ident_bf16[:], rhs=noise_sb[:], start=True, stop=True
+                parked["noise"][:], lhsT=ident_bf16[:], rhs=noise_sb[:], start=True, stop=True
             )
 
         x_words = x_sb[:].rearrange("b t k -> b (t k)").bitcast(F32)
@@ -260,7 +272,7 @@ def tile_lstmlayer_kernel(
         GATE_BUFS = {GATE_F: ROUNDS, GATE_I: 3, GATE_G: 2}
 
         def turn_input(r):
-            turned[r] = product_psum.tile([P, STEPS, 2, P], F32, tag="product", name="turned")
+            turned[r] = parked_psum.tile([P, STEPS, 2, P], F32, tag="parked", name="turned")
             for s in range(STEPS):
                 row = (r * STEPS + s) * WORDS
                 for u in range(2):
@@ -370,7 +382,7 @@ def tile_lstmlayer_kernel(
             nc.vector.tensor_tensor(
                 out=part,
                 in0=part,
-                in1=c0_parked[:, first:, :].unsqueeze(2).to_broadcast([P, CHUNKS - first, STEPS, P]),
+                in1=parked["c0"][:, first:, :].unsqueeze(2).to_broadcast([P, CHUNKS - first, STEPS, P]),
                 op=ALU.mult,
             )
 
@@ -430,7 +442,10 @@ def tile_lstmlayer_kernel(
 
         def add_noise_and_store(r):
             nc.vector.tensor_tensor(
-                out=gates[(r, GATE_O)][:], in0=gates[(r, GATE_O)][:], in1=noise_each_step, op=ALU.add
+                out=gates[(r, GATE_O)][:],
+                in0=gates[(r, GATE_O)][:],
+                in1=parked["noise"][:].unsqueeze(1).to_broadcast([P, STEPS, H]),
+                op=ALU.add,
             )
             nc.sync.dma_start(
                 out=h_out[r * STEPS : (r + 1) * STEPS].rearrange("t b n -> b t n"),
@@ -443,9 +458,6 @@ def tile_lstmlayer_kernel(
             if 0 <= r < ROUNDS:
                 stage_of_round(r)
 
-        noise_parked = parked_psum.tile([P, H], F32)
-        noise_each_step = noise_parked[:].unsqueeze(1).to_broadcast([P, STEPS, H])
-        c0_parked = parked_psum.tile([P, CHUNKS, P], F32)
         idle_sum = product_psum.tile([P, H], F32, tag="product")
         for i in range(WARM_UP):
             nc.tensor.matmul(idle_sum[:], lhsT=ones[:], rhs=zeros[:], start=True, stop=True)
@@ -472,11 +484,12 @@ def tile_lstmlayer_kernel(
             8: [lambda: sum_fixed_turned(GATE_G, 1)],
             12: [lambda: transpose_whh(GATE_O, 0)],
             13: [lambda: transpose_whh(GATE_O, 1)],
+            14: [park_c0],
         }
         for r in range(ROUNDS):
             multiply_input_turned(r, GATE_F)
             if r == 0:
-                turn_c0()
+                turn_c0_for_gpsimd()
             add_turned_gate(r, GATE_F)
             if r == 0:
                 activate_turned_gate(r, GATE_F)

@@ -35,7 +35,7 @@ STEPS = 2
 ROUNDS = T // STEPS
 PAIRS = ROUNDS // 2
 LOAD_STEPS = 4
-GPSIMD_CHUNKS = (2, 2)
+GPSIMD_CHUNKS = (3, 2)
 VECTOR_ROUNDS = 1
 WARM_UP = 6
 

@@ -37,7 +37,7 @@ PAIRS = ROUNDS // 2
 LOAD_STEPS = 4
 GPSIMD_CHUNKS = (3, 2)
 VECTOR_ROUNDS = 1
-WARM_UP = 6
+WARM_UP = 3
 
 FLOPS = 2 * T * P * K * N + 2 * P * H * N
 
@@ -404,8 +404,11 @@ def tile_lstmlayer_kernel(
                 op=ALU.mult,
             )
 
+        def steps_in_order(r):
+            return tuple(reversed(range(STEPS))) if r == ROUNDS - 1 else tuple(range(STEPS))
+
         def sum_cell(r):
-            for s in range(STEPS):
+            for s in steps_in_order(r):
                 cell[(r, s)] = cell_psum.tile([P, H], F32, tag="cell", name="cell")
                 for j in range(CHUNKS):
                     cols = slice(j * P, (j + 1) * P)
@@ -428,7 +431,7 @@ def tile_lstmlayer_kernel(
 
         def squash_cell(r):
             squashed[r] = work.tile([P, STEPS, H], F32, name="squashed", tag="squashed", bufs=3)
-            for s in range(STEPS):
+            for s in steps_in_order(r):
                 nc.scalar.activation(out=squashed[r][:, s, :], in_=cell[(r, s)][:], func=ACT.Tanh)
             if r == ROUNDS - 1:
                 last_cell = keep.tile([P, H], F32)
@@ -451,8 +454,21 @@ def tile_lstmlayer_kernel(
                 out=h_out[r * STEPS : (r + 1) * STEPS].rearrange("t b n -> b t n"),
                 in_=gates[(r, GATE_O)][:],
             )
-            if r == ROUNDS - 1:
-                nc.sync.dma_start(out=state_out[0], in_=gates[(r, GATE_O)][:, STEPS - 1, :])
+
+        def finish_last_round():
+            r = ROUNDS - 1
+            out_gate = gates[(r, GATE_O)]
+            for s in steps_in_order(r):
+                nc.vector.tensor_tensor(
+                    out=out_gate[:, s, :], in0=out_gate[:, s, :], in1=squashed[r][:, s, :], op=ALU.mult
+                )
+            for s in steps_in_order(r):
+                nc.vector.tensor_tensor(
+                    out=out_gate[:, s, :], in0=out_gate[:, s, :], in1=parked["noise"][:], op=ALU.add
+                )
+                nc.sync.dma_start(out=h_out[r * STEPS + s], in_=out_gate[:, s, :])
+                if s == STEPS - 1:
+                    nc.sync.dma_start(out=state_out[0], in_=out_gate[:, s, :])
 
         def run(stage_of_round, r):
             if 0 <= r < ROUNDS:
@@ -525,10 +541,10 @@ def tile_lstmlayer_kernel(
             if m + 1 < ROUNDS:
                 multiply_input_turned(m + 1, GATE_I)
             run(sum_cell, m - 1)
-            if on_vector(m - 2):
+            if m - 2 == ROUNDS - 1:
                 run(add_noise_and_store, m - 3)
-                run(multiply_o, m - 2)
-            else:
+                finish_last_round()
+            elif m - 2 < ROUNDS - 1:
                 run(multiply_o, m - 2)
                 run(add_noise_and_store, m - 3)
             run(squash_cell, m - 1)

@@ -523,12 +523,12 @@ def tile_lstmlayer_kernel(
             run(multiply_f_c0, r - 1)
 
         multiply_input_turned(0, GATE_I)
+        multiply_input_turned(0, GATE_G)
         for m in range(ROUNDS + 3):
             run(multiply_i_g, m - 1)
             if m < ROUNDS:
                 add_turned_gate(m, GATE_I)
                 activate_turned_gate(m, GATE_I)
-                multiply_input_turned(m, GATE_G)
                 add_turned_gate(m, GATE_G)
                 activate_turned_gate(m, GATE_G)
             if m == 0:
@@ -540,6 +540,7 @@ def tile_lstmlayer_kernel(
             run(multiply_f_c0_on_vector, m)
             if m + 1 < ROUNDS:
                 multiply_input_turned(m + 1, GATE_I)
+                multiply_input_turned(m + 1, GATE_G)
             run(sum_cell, m - 1)
             if m - 2 == ROUNDS - 1:
                 run(add_noise_and_store, m - 3)

@@ -502,7 +502,7 @@ def tile_lstmlayer_kernel(
             13: [lambda: transpose_whh(GATE_O, 1)],
             14: [park_c0],
         }
-        for r in range(ROUNDS):
+        for r in range(ROUNDS - 1):
             multiply_input_turned(r, GATE_F)
             if r == 0:
                 turn_c0_for_gpsimd()
@@ -526,13 +526,18 @@ def tile_lstmlayer_kernel(
         multiply_input_turned(0, GATE_G)
         for m in range(ROUNDS + 3):
             run(multiply_i_g, m - 1)
+            if m == 1:
+                multiply_f_c0(ROUNDS - 1)
             if m < ROUNDS:
                 add_turned_gate(m, GATE_I)
                 activate_turned_gate(m, GATE_I)
                 add_turned_gate(m, GATE_G)
                 activate_turned_gate(m, GATE_G)
             if m == 0:
-                multiply_f_c0(ROUNDS - 1)
+                multiply_input_turned(ROUNDS - 1, GATE_F)
+                add_turned_gate(ROUNDS - 1, GATE_F)
+                activate_turned_gate(ROUNDS - 1, GATE_F)
+                multiply_f_c0(ROUNDS - 2)
                 sum_fixed_o()
                 park_noise()
             run(multiply_input_o, m - 1)

from contextlib import ExitStack

import concourse.mybir as mybir
from concourse.masks import make_identity

F32 = mybir.dt.float32
BF16 = mybir.dt.bfloat16
U8 = mybir.dt.uint8
U32 = mybir.dt.uint32
I32 = mybir.dt.int32
FP8X4 = mybir.dt.float8_e4m3fn_x4
ACT = mybir.ActivationFunctionType
ALU = mybir.AluOpType

T = 32
P = 128
K = 512
H = 512
GATES = 4
GATE_I = 0
GATE_F = 1
GATE_G = 2
GATE_O = 3
TURNED_GATES = (GATE_F, GATE_I, GATE_G)
GATE_FUNC = {GATE_I: ACT.Sigmoid, GATE_F: ACT.Sigmoid, GATE_G: ACT.Tanh, GATE_O: ACT.Sigmoid}
N = GATES * H
CHUNKS = H // P
ALL_CHUNKS = GATES * CHUNKS
HALVES = 2
WORDS = K // 2
H_WORDS = H // 2
WORD_CHUNKS = H_WORDS // P
ROW_BLOCKS = H // P
STEPS = 2
ROUNDS = T // STEPS
PAIRS = ROUNDS // 2
LOAD_STEPS = 4
GPSIMD_CHUNKS = (3, 2)
VECTOR_ROUNDS = 1
WARM_UP = 3

FLOPS = 2 * T * P * K * N + 2 * P * H * N


def tile_lstmlayer_kernel(
    tc, x, h0, c0, noise, w_ih_words, w_ih_scales, w_hh, b_ih, b_hh, h_out, state_out
):
    nc = tc.nc
    with ExitStack() as ctx:
        ctx.enter_context(tc.manual_schedule())
        keep = ctx.enter_context(tc.tile_pool(name="keep", bufs=1))
        stage = ctx.enter_context(tc.tile_pool(name="stage", bufs=2))
        work = ctx.enter_context(tc.tile_pool(name="work", bufs=2))
        parked_psum = ctx.enter_context(tc.psum_pool(name="parked_psum", bufs=2))
        cell_psum = ctx.enter_context(tc.psum_pool(name="cell_psum", bufs=2))
        product_psum = ctx.enter_context(tc.psum_pool(name="product_psum", bufs=4))

        ident_f32 = keep.tile([P, P], F32)
        make_identity(nc, ident_f32[:])
        ident_bf16 = keep.tile([P, P], BF16)
        make_identity(nc, ident_bf16[:])
        ones = keep.tile([P, P], BF16)
        nc.vector.memset(ones[:], 1.0)
        zeros = keep.tile([P, H], BF16)
        nc.vector.memset(zeros[:], 0.0)
        table_warmer = keep.tile([P, 1], F32)
        nc.scalar.activation(out=table_warmer[:], in_=ones[:, 0:1], func=ACT.Sigmoid)
        w_scales = keep.tile([P, N], U8, align_bytes=64)
        nc.vector.memset(w_scales[:].bitcast(I32), 0)
        bias_sb = keep.tile([P, P], BF16)
        nc.vector.memset(bias_sb[:], 0.0)
        pick = keep.tile([P, ALL_CHUNKS], BF16)
        nc.vector.tensor_tensor(
            out=pick[:],
            in0=ident_bf16[:, 0:ALL_CHUNKS],
            in1=ident_bf16[:, ALL_CHUNKS : 2 * ALL_CHUNKS],
            op=ALU.add,
        )

        h0_sb = keep.tile([P, H], BF16)
        c0_sb = keep.tile([P, H], BF16)
        noise_sb = keep.tile([P, H], BF16)
        whh_sb = {}
        w_codes = keep.tile([P, N], U32, align_bytes=64)
        w_words_flat = w_ih_words[0].rearrange("p n t -> p (n t)").bitcast(I32)
        x_sb = keep.tile([P, T, K], BF16)

        def load_whh(g, pieces):
            whh_sb[g] = stage.tile([P, ROW_BLOCKS, H], BF16, name="whh_sb", tag="whh_sb")
            blocks = ROW_BLOCKS // pieces
            for piece in range(pieces):
                first = piece * blocks
                nc.sync.dma_start(
                    out=whh_sb[g][:, first : first + blocks, :],
                    in_=w_hh[g * H + first * P : g * H + (first + blocks) * P, :].rearrange(
                        "(j p) k -> p j k", p=P
                    ),
                )

        def load_w_codes(g):
            nc.sync.dma_start(
                out=w_codes[:, g * H : (g + 1) * H].bitcast(I32),
                in_=w_words_flat[:, g * H : (g + 1) * H],
            )

        def load_x(first, count):
            nc.sync.dma_start(
                out=x_sb[:, first : first + count, :],
                in_=x[first : first + count].rearrange("t b k -> b t k"),
            )

        def load_scales(first_gate, gates_loaded):
            cols = slice(first_gate * H, (first_gate + gates_loaded) * H)
            for quadrant in range(4):
                nc.sync.dma_start(
                    out=w_scales[32 * quadrant : 32 * quadrant + 4, cols].bitcast(I32),
                    in_=w_ih_scales[0, 4 * quadrant : 4 * quadrant + 4, cols].bitcast(I32),
                )

        load_x(0, STEPS)
        nc.sync.dma_start(out=h0_sb[:], in_=h0)
        load_whh(GATE_F, 2)
        nc.sync.dma_start(
            out=bias_sb[0:ALL_CHUNKS, :], in_=b_ih.rearrange("(c n) -> c n", c=ALL_CHUNKS)
        )
        nc.sync.dma_start(
            out=bias_sb[ALL_CHUNKS : 2 * ALL_CHUNKS, :], in_=b_hh.rearrange("(c n) -> c n", c=ALL_CHUNKS)
        )
        load_x(STEPS, STEPS)
        load_w_codes(GATE_F)
        load_scales(GATE_F, 1)
        nc.sync.dma_start(out=c0_sb[:], in_=c0)
        load_x(4, LOAD_STEPS)
        load_whh(GATE_I, 1)
        load_x(8, LOAD_STEPS)
        load_w_codes(GATE_I)
        load_scales(GATE_I, 1)
        load_whh(GATE_G, 1)
        load_x(12, LOAD_STEPS)
        load_w_codes(GATE_G)
        load_scales(GATE_G, 2)
        load_x(16, LOAD_STEPS)
        load_x(20, LOAD_STEPS)
        load_whh(GATE_O, 1)
        load_x(24, LOAD_STEPS)
        load_w_codes(GATE_O)
        load_x(28, LOAD_STEPS)
        nc.sync.dma_start(out=noise_sb[:], in_=noise)

        h0_words = h0_sb[:].bitcast(F32)
        h0T = keep.tile([P, WORD_CHUNKS, 2 * P], BF16)
        whhT = keep.tile([P, WORD_CHUNKS, 2 * N], BF16)
        fixedT = keep.tile([P, len(TURNED_GATES), CHUNKS, P], F32)
        fixed_o = keep.tile([P, H], F32)
        c0T = keep.tile([P, CHUNKS, P], F32)

        def spare_bank(shape, early):
            if early:
                return product_psum.tile(shape, F32, tag="product", name="spare")
            return cell_psum.tile(shape, F32, tag="cell", name="spare")

        def transpose_h0():
            h0_turned = product_psum.tile([P, WORD_CHUNKS, P], F32, tag="product")
            for w in range(WORD_CHUNKS):
                nc.tensor.transpose(
                    h0_turned[:, w, :], h0_words[:, w * P : (w + 1) * P], ident_f32[:]
                )
            nc.vector.tensor_copy(
                out=h0T[:].rearrange("q w c -> q (w c)").bitcast(F32),
                in_=h0_turned[:].rearrange("q w b -> q (w b)"),
            )

        def transpose_whh(g, half, early=False):
            whh_words = whh_sb[g][:].rearrange("p j k -> p (j k)").bitcast(F32)
            blocks = ROW_BLOCKS // HALVES
            n0 = g * H + half * blocks * P
            for w in range(WORD_CHUNKS):
                whh_turned = spare_bank([P, blocks, P], early)
                for jj in range(blocks):
                    first_word = (half * blocks + jj) * H_WORDS + w * P
                    nc.tensor.transpose(
                        whh_turned[:, jj, :], whh_words[:, first_word : first_word + P], ident_f32[:]
                    )
                copy = nc.scalar.copy if (w == 1 and g == GATE_F) else nc.vector.tensor_copy
                copy(
                    out=whhT[:, w, 2 * n0 : 2 * (n0 + blocks * P)].bitcast(F32),
                    in_=whh_turned[:].rearrange("q j n -> q (j n)"),
                )

        def sum_fixed_turned(g, half):
            chunks = CHUNKS // HALVES
            fixed_sum = spare_bank([P, chunks, P], False)
            for jj in range(chunks):
                n0 = g * H + (half * chunks + jj) * P
                for w in range(WORD_CHUNKS):
                    for e in range(2):
                        nc.tensor.matmul(
                            fixed_sum[:, jj, :],
                            lhsT=whhT[:, w, 2 * n0 + e : 2 * (n0 + P) : 2],
                            rhs=h0T[:, w, e : 2 * P : 2],
                            start=(w == 0 and e == 0),
                            stop=False,
                        )
                c = n0 // P
                nc.tensor.matmul(
                    fixed_sum[:, jj, :],
                    lhsT=bias_sb[:],
                    rhs=pick[:, c : c + 1].to_broadcast([P, P]),
                    start=False,
                    stop=True,
                )
            copy = nc.scalar.copy if g == GATE_F else nc.vector.tensor_copy
            copy(
                out=fixedT[:, TURNED_GATES.index(g), half * chunks : (half + 1) * chunks],
                in_=fixed_sum[:],
            )

        def sum_fixed_o():
            fixed_sum = spare_bank([P, CHUNKS, P], False)
            for j in range(CHUNKS):
                n0 = GATE_O * H + j * P
                for w in range(WORD_CHUNKS):
                    for e in range(2):
                        nc.tensor.matmul(
                            fixed_sum[:, j, :],
                            lhsT=h0T[:, w, e : 2 * P : 2],
                            rhs=whhT[:, w, 2 * n0 + e : 2 * (n0 + P) : 2],
                            start=(w == 0 and e == 0),
                            stop=False,
                        )
                c = n0 // P
                nc.tensor.matmul(
                    fixed_sum[:, j, :],
                    lhsT=pick[:, c : c + 1].to_broadcast([P, P]),
                    rhs=bias_sb[:],
                    start=False,
                    stop=True,
                )
            nc.scalar.copy(out=fixed_o[:], in_=fixed_sum[:].rearrange("b j n -> b (j n)"))

        parked = {}

        def turn_c0(bank, chunks):
            for j in range(chunks):
                nc.tensor.matmul(
                    bank[:, j, :],
                    lhsT=c0_sb[:, j * P : (j + 1) * P],
                    rhs=ident_bf16[:],
                    start=True,
                    stop=True,
                )

        def turn_c0_for_gpsimd():
            chunks = max(GPSIMD_CHUNKS)
            bank = spare_bank([P, chunks, P], False)
            turn_c0(bank, chunks)
            nc.scalar.copy(out=c0T[:, :chunks], in_=bank[:])

        def park_c0():
            parked["c0"] = parked_psum.tile([P, CHUNKS, P], F32, tag="parked", name="c0_parked")
            turn_c0(parked["c0"], CHUNKS)

        def park_noise():
            parked["noise"] = parked_psum.tile([P, H], F32, tag="parked", name="noise_parked")
            nc.tensor.matmul(
                parked["noise"][:], lhsT=ident_bf16[:], rhs=noise_sb[:], start=True, stop=True
            )

        x_words = x_sb[:].rearrange("b t k -> b (t k)").bitcast(F32)
        turned, grouped, x_codes, x_scales = {}, {}, {}, {}
        products, gates, cell, squashed = {}, {}, {}, {}
        GATE_BUFS = {GATE_F: ROUNDS, GATE_I: 3, GATE_G: 2}

        def turn_input(r):
            turned[r] = parked_psum.tile([P, STEPS, 2, P], F32, tag="parked", name="turned")
            for s in range(STEPS):
                row = (r * STEPS + s) * WORDS
                for u in range(2):
                    nc.tensor.transpose(
                        turned[r][:, s, u, :], x_words[:, row + u : row + WORDS : 2], ident_f32[:]
                    )

        def group_input(r):
            if r % 2 == 0:
                grouped[r // 2] = stage.tile(
                    [P, 2, STEPS * K], BF16, align_bytes=64, name="grouped", tag="grouped"
                )
            nc.scalar.copy(
                out=grouped[r // 2][:, r % 2, :]
                .bitcast(F32)
                .rearrange("p (s b u) -> p s b u", s=STEPS, u=2),
                in_=turned[r][:].rearrange("p s u b -> p s b u"),
            )

        def quantise_input(pair, rounds):
            if pair not in x_codes:
                x_codes[pair] = stage.tile(
                    [P, 2, STEPS * P], U32, align_bytes=64, name="x_codes", tag="x_codes", bufs=PAIRS
                )
                x_scales[pair] = stage.tile(
                    [P, 2, STEPS * P], U8, align_bytes=64, name="x_scales", tag="x_scales", bufs=PAIRS
                )
            nc.vector.quantize_mx(
                out=x_codes[pair][:, rounds, :].rearrange("p r c -> p (r c)").bitcast(FP8X4),
                scales=x_scales[pair][:, rounds, :].rearrange("p r c -> p (r c)"),
                in_=grouped[pair][:, rounds, :].rearrange("p r c -> p (r c)"),
            )

        def multiply_input_turned(r, g):
            for half in range(HALVES):
                product = product_psum.tile([P, H], F32, tag="product", name="product")
                products[(r, g, half)] = product
                for jj in range(2):
                    n0 = g * H + (2 * half + jj) * P
                    nc.tensor.matmul_mx(
                        out=product[:, jj * STEPS * P : (jj + 1) * STEPS * P],
                        lhsT=w_codes[:, n0 : n0 + P].bitcast(FP8X4),
                        lhsT_scale=w_scales[:, n0 : n0 + P],
                        rhs=x_codes[r // 2][:, r % 2, :].bitcast(FP8X4),
                        rhs_scale=x_scales[r // 2][:, r % 2, :],
                        start=True,
                        stop=True,
                    )

        def add_turned_gate(r, g):
            gate = work.tile(
                [P, CHUNKS, STEPS, P], F32, name="gate", tag="gate%d" % g, bufs=GATE_BUFS[g]
            )
            gates[(r, g)] = gate
            slot = TURNED_GATES.index(g)
            for half in range(HALVES):
                nc.vector.tensor_tensor(
                    out=gate[:, 2 * half : 2 * half + 2],
                    in0=products[(r, g, half)][:].rearrange("q (j s b) -> q j s b", j=2, s=STEPS),
                    in1=fixedT[:, slot, 2 * half : 2 * half + 2, :]
                    .unsqueeze(2)
                    .to_broadcast([P, 2, STEPS, P]),
                    op=ALU.add,
                )

        def activate_turned_gate(r, g):
            flat = gates[(r, g)][:].rearrange("q j s b -> q (j s b)")
            nc.scalar.activation(out=flat, in_=flat, func=GATE_FUNC[g])

        def multiply_input_o(r):
            cols = slice(GATE_O * H, (GATE_O + 1) * H)
            for s in range(STEPS):
                rows = slice(s * P, (s + 1) * P)
                products[(r, GATE_O, s)] = product_psum.tile([P, H], F32, tag="product", name="product_o")
                nc.tensor.matmul_mx(
                    out=products[(r, GATE_O, s)][:],
                    lhsT=x_codes[r // 2][:, r % 2, rows].bitcast(FP8X4),
                    lhsT_scale=x_scales[r // 2][:, r % 2, rows],
                    rhs=w_codes[:, cols].bitcast(FP8X4),
                    rhs_scale=w_scales[:, cols],
                    start=True,
                    stop=True,
                )

        def make_o(r):
            gates[(r, GATE_O)] = work.tile([P, STEPS, H], F32, name="gate_o", tag="gate_o", bufs=5)
            for s in range(STEPS):
                nc.vector.tensor_tensor(
                    out=gates[(r, GATE_O)][:, s, :],
                    in0=products[(r, GATE_O, s)][:],
                    in1=fixed_o[:],
                    op=ALU.add,
                )
            nc.scalar.activation(
                out=gates[(r, GATE_O)][:], in_=gates[(r, GATE_O)][:], func=GATE_FUNC[GATE_O]
            )

        def on_vector(r):
            return r >= ROUNDS - VECTOR_ROUNDS

        def helper(r):
            return nc.vector if on_vector(r) else nc.gpsimd

        def multiply_f_c0_on_vector(r):
            first = GPSIMD_CHUNKS[r % 2]
            part = gates[(r, GATE_F)][:, first:]
            nc.vector.tensor_tensor(
                out=part,
                in0=part,
                in1=parked["c0"][:, first:, :].unsqueeze(2).to_broadcast([P, CHUNKS - first, STEPS, P]),
                op=ALU.mult,
            )

        def multiply_f_c0(r):
            chunks = GPSIMD_CHUNKS[r % 2]
            part = gates[(r, GATE_F)][:, :chunks]
            nc.gpsimd.tensor_tensor(
                out=part,
                in0=part,
                in1=c0T[:, :chunks, :].unsqueeze(2).to_broadcast([P, chunks, STEPS, P]),
                op=ALU.mult,
            )

        def multiply_i_g(r):
            helper(r).tensor_tensor(
                out=gates[(r, GATE_I)][:],
                in0=gates[(r, GATE_I)][:],
                in1=gates[(r, GATE_G)][:],
                op=ALU.mult,
            )

        def steps_in_order(r):
            return tuple(reversed(range(STEPS))) if r == ROUNDS - 1 else tuple(range(STEPS))

        def sum_cell(r):
            for s in steps_in_order(r):
                cell[(r, s)] = cell_psum.tile([P, H], F32, tag="cell", name="cell")
                for j in range(CHUNKS):
                    cols = slice(j * P, (j + 1) * P)
                    nc.tensor.matmul(
                        cell[(r, s)][:, cols],
                        lhsT=gates[(r, GATE_F)][:, j, s, :],
                        rhs=ident_f32[:],
                        is_transpose=True,
                        start=True,
                        stop=False,
                    )
                    nc.tensor.matmul(
                        cell[(r, s)][:, cols],
                        lhsT=gates[(r, GATE_I)][:, j, s, :],
                        rhs=ident_f32[:],
                        is_transpose=True,
                        start=False,
                        stop=True,
                    )

        def squash_cell(r):
            squashed[r] = work.tile([P, STEPS, H], F32, name="squashed", tag="squashed", bufs=3)
            for s in steps_in_order(r):
                nc.scalar.activation(out=squashed[r][:, s, :], in_=cell[(r, s)][:], func=ACT.Tanh)
            if r == ROUNDS - 1:
                last_cell = keep.tile([P, H], F32)
                nc.scalar.copy(out=last_cell[:], in_=cell[(r, STEPS - 1)][:])
                nc.sync.dma_start(out=state_out[1], in_=last_cell[:])

        def multiply_o(r):
            helper(r).tensor_tensor(
                out=gates[(r, GATE_O)][:], in0=gates[(r, GATE_O)][:], in1=squashed[r][:], op=ALU.mult
            )

        def add_noise_and_store(r):
            nc.vector.tensor_tensor(
                out=gates[(r, GATE_O)][:],
                in0=gates[(r, GATE_O)][:],
                in1=parked["noise"][:].unsqueeze(1).to_broadcast([P, STEPS, H]),
                op=ALU.add,
            )
            nc.sync.dma_start(
                out=h_out[r * STEPS : (r + 1) * STEPS].rearrange("t b n -> b t n"),
                in_=gates[(r, GATE_O)][:],
            )

        def finish_last_round():
            r = ROUNDS - 1
            out_gate = gates[(r, GATE_O)]
            for s in steps_in_order(r):
                nc.vector.tensor_tensor(
                    out=out_gate[:, s, :], in0=out_gate[:, s, :], in1=squashed[r][:, s, :], op=ALU.mult
                )
            for s in steps_in_order(r):
                nc.vector.tensor_tensor(
                    out=out_gate[:, s, :], in0=out_gate[:, s, :], in1=parked["noise"][:], op=ALU.add
                )
                nc.sync.dma_start(out=h_out[r * STEPS + s], in_=out_gate[:, s, :])
                if s == STEPS - 1:
                    nc.sync.dma_start(out=state_out[0], in_=out_gate[:, s, :])

        def run(stage_of_round, r):
            if 0 <= r < ROUNDS:
                stage_of_round(r)

        idle_sum = product_psum.tile([P, H], F32, tag="product")
        for i in range(WARM_UP):
            nc.tensor.matmul(idle_sum[:], lhsT=ones[:], rhs=zeros[:], start=True, stop=True)
        turn_input(0)
        group_input(0)
        transpose_h0()
        transpose_whh(GATE_F, 0)
        transpose_whh(GATE_F, 1, early=True)
        quantise_input(0, slice(0, 1))
        turn_input(1)
        group_input(1)
        quantise_input(0, slice(1, 2))
        sum_fixed_turned(GATE_F, 0)
        sum_fixed_turned(GATE_F, 1)

        between = {
            1: [lambda: transpose_whh(GATE_I, 0)],
            2: [lambda: transpose_whh(GATE_I, 1)],
            3: [lambda: sum_fixed_turned(GATE_I, 0)],
            4: [lambda: sum_fixed_turned(GATE_I, 1)],
            5: [lambda: transpose_whh(GATE_G, 0)],
            6: [lambda: transpose_whh(GATE_G, 1)],
            7: [lambda: sum_fixed_turned(GATE_G, 0)],
            8: [lambda: sum_fixed_turned(GATE_G, 1)],
            12: [lambda: transpose_whh(GATE_O, 0)],
            13: [lambda: transpose_whh(GATE_O, 1)],
            14: [park_c0],
        }
        for r in range(ROUNDS - 1):
            multiply_input_turned(r, GATE_F)
            if r == 0:
                turn_c0_for_gpsimd()
            add_turned_gate(r, GATE_F)
            if r == 0:
                activate_turned_gate(r, GATE_F)
            for ahead in ((2, 3), (4, 5))[r] if r < 2 else (r + 4,):
                run(turn_input, ahead)
                run(group_input, ahead)
            if r > 0:
                activate_turned_gate(r, GATE_F)
            if r == 1:
                quantise_input(1, slice(0, 2))
            if r % 2 == 0 and 2 <= r and r + 3 < ROUNDS:
                quantise_input((r + 2) // 2, slice(0, 2))
            for task in between.get(r, []):
                task()
            run(multiply_f_c0, r - 1)

        multiply_input_turned(0, GATE_I)
        multiply_input_turned(0, GATE_G)
        for m in range(ROUNDS + 3):
            run(multiply_i_g, m - 1)
            if m == 1:
                multiply_f_c0(ROUNDS - 1)
            if m < ROUNDS:
                add_turned_gate(m, GATE_I)
                activate_turned_gate(m, GATE_I)
                add_turned_gate(m, GATE_G)
                activate_turned_gate(m, GATE_G)
            if m == 0:
                multiply_input_turned(ROUNDS - 1, GATE_F)
                add_turned_gate(ROUNDS - 1, GATE_F)
                activate_turned_gate(ROUNDS - 1, GATE_F)
                multiply_f_c0(ROUNDS - 2)
                sum_fixed_o()
                park_noise()
            run(multiply_input_o, m - 1)
            run(make_o, m - 1)
            run(multiply_f_c0_on_vector, m)
            if m + 1 < ROUNDS:
                multiply_input_turned(m + 1, GATE_I)
                multiply_input_turned(m + 1, GATE_G)
            run(sum_cell, m - 1)
            if m - 2 == ROUNDS - 1:
                run(add_noise_and_store, m - 3)
                finish_last_round()
            elif m - 2 < ROUNDS - 1:
                run(multiply_o, m - 2)
                run(add_noise_and_store, m - 3)
            run(squash_cell, m - 1)
